import numpy as np
import ml_dtypes


def mxq(x, axis, fmt="e4m3"):
    dtype, down = {"e4m3": (ml_dtypes.float8_e4m3fn, 7), "e5m2": (ml_dtypes.float8_e5m2, 14)}[fmt]
    v = np.moveaxis(np.asarray(x, np.float32).astype(ml_dtypes.bfloat16).astype(np.float64), axis, -1)
    blocks = v.reshape(v.shape[:-1] + (-1, 32))
    amax = np.abs(blocks).max(-1, keepdims=True)
    byte = np.maximum(np.where(amax > 0, np.frexp(amax)[1] - 1 + 127, 0) - down, 1)
    scale = np.exp2(byte - 127.0)
    codes = (blocks / scale).astype(np.float32).astype(dtype).astype(np.float64)
    return np.moveaxis((codes * scale).reshape(v.shape), -1, axis)


WIDE = False


def mx_kscale(k):
    if not WIDE:
        return np.ones(k)
    levels = np.array([10, -10, 5, -5, 0])
    if k % 512:
        return np.exp2(np.random.permutation(np.resize(levels, k // 32))).repeat(32)
    a = np.empty((k // 512, 16))
    for p in range(k // 512):
        a[p, :8] = np.random.permutation(np.resize(levels, 8))
        for g in range(8):
            far = levels[np.abs(levels - a[p, g]) >= 10]
            a[p, g + 8] = far[np.random.randint(len(far))]
    return np.exp2(a.ravel()).repeat(32)


BF16 = ml_dtypes.bfloat16


def bf(x):
    return np.asarray(x, np.float32).astype(BF16)


def f64(x):
    return np.asarray(x).astype(np.float64)


S, A, B, K, H, G = 32, 8, 16, 512, 256, 3


def sigmoid(v):
    return 1.0 / (1.0 + np.exp(-v))


def setup_inputs():
    s = mx_kscale(K)
    c = 0.7 / np.sqrt(K)
    return {"x": bf(np.random.standard_normal((S + 1, A, B, K)) * s),
            "x_mix": bf(np.random.standard_normal((S + 1, A, B, H))),
            "WL": bf(np.random.standard_normal((H, K)) * c / s),
            "WR": bf(np.random.standard_normal((H, K)) * c / s),
            "GL": bf(np.random.standard_normal((G * H, K)) * c / s),
            "GR": bf(np.random.standard_normal((G * H, K)) * c / s)}


def reference(x, x_mix, WL, WR, GL, GR):
    xm = f64(x_mix)
    left, right = xm[:-1], xm[1:]
    xq = mxq(f64(x), 3, "e4m3")
    lq, rq = xq[:-1], xq[1:]
    center = sigmoid((lq @ mxq(f64(WL), 1, "e4m3").T) + (rq @ mxq(f64(WR), 1, "e4m3").T))
    gate = (lq @ mxq(f64(GL), 1, "e4m3").T) + (rq @ mxq(f64(GR), 1, "e4m3").T)
    g = gate.reshape(gate.shape[:-1] + (G, H))
    e = np.exp(g - g.max(-2, keepdims=True))
    w = e / e.sum(-2, keepdims=True)
    return left * w[..., 0, :] + right * w[..., 1, :] + center * w[..., 2, :]

@@ -1,0 +1,320 @@
+from contextlib import ExitStack
+
+import concourse.mybir as mybir
+from concourse.masks import make_identity
+
+F32 = mybir.dt.float32
+BF16 = mybir.dt.bfloat16
+U32 = mybir.dt.uint32
+U8 = mybir.dt.uint8
+FP8X4 = mybir.dt.float8_e4m3fn_x4
+AF = mybir.ActivationFunctionType
+ALU = mybir.AluOpType
+
+P = 128
+K = 512
+H = 256
+POSITIONS = 32
+BLOCKS = POSITIONS + 1
+PAIR_COLS = 2 * H
+PAIRS = POSITIONS // 2
+GROUP_PAIRS = 2
+GROUP_POSITIONS = 2 * GROUP_PAIRS
+GROUP_COLS = GROUP_PAIRS * PAIR_COLS
+GROUPS = PAIRS // GROUP_PAIRS
+ROUND = 4
+PIECE_BLOCKS = 2
+UNIT_BLOCKS = GROUP_POSITIONS
+UNITS = GROUPS + 1
+LEAD = 3
+FLOOR = 40.0
+PSUM_BANKS = 8
+
+LEFT, RIGHT = 0, 1
+OPERANDS = ("centre", "g0", "g1", "neg_g1", "neg_g2")
+CHUNK_USES = {"centre": ("centre", None), "g0": ("g0", None), "g1": ("g1", "neg_g1"), "g2": (None, "neg_g2")}
+GATE_CHUNK = {"g0": 0, "g1": 1, "g2": 2}
+
+FLOPS = 2 * POSITIONS * P * (2 * K) * (4 * H)
+
+
+def tile_grconv_pa_t_kernel(tc, x, x_mix, WL, WR, GL, GR, out):
+    nc = tc.nc
+    x_rows = x.rearrange("s a b k -> (a b) s k")
+    mix_rows = x_mix.rearrange("s a b h -> (a b) s h")
+    out_rows = out.rearrange("s a b h -> (a b) s h")
+    centres = (WL, WR)
+    gates = (GL, GR)
+
+    with ExitStack() as ctx:
+        ctx.enter_context(tc.manual_schedule())
+        const = ctx.enter_context(tc.tile_pool(name="const", bufs=1))
+        resident = ctx.enter_context(tc.tile_pool(name="resident", bufs=1))
+        stage = ctx.enter_context(tc.tile_pool(name="stage", bufs=3))
+        keep = ctx.enter_context(tc.tile_pool(name="keep", bufs=ROUND + 1))
+        psum = ctx.enter_context(tc.psum_pool(name="psum", bufs=1))
+
+        plus_floor = const.tile([P, 1], F32)
+        nc.vector.memset(plus_floor[:], FLOOR)
+        minus_floor = const.tile([P, 1], F32)
+        nc.vector.memset(minus_floor[:], -FLOOR)
+        warm = const.tile([P, 1], F32)
+        nc.scalar.activation(out=warm[:], in_=plus_floor[:], func=AF.Sigmoid)
+        ident_words = const.tile([P, P], F32)
+        make_identity(nc, ident_words[:])
+        ident = const.tile([P, P], BF16)
+        make_identity(nc, ident[:])
+        neg_ident = const.tile([P, P], BF16)
+        nc.vector.tensor_scalar_mul(out=neg_ident[:], in0=ident[:], scalar1=-1.0)
+
+        x_nat = resident.tile([P, BLOCKS, K], BF16)
+        mix_in = resident.tile([P, BLOCKS, H], BF16)
+        x_codes = resident.tile([P, BLOCKS, P], U32, align_bytes=64)
+        x_scales = resident.tile([P, BLOCKS, P], U8, align_bytes=64)
+        w_codes = resident.tile([P, 2 * len(OPERANDS), H], U32, align_bytes=64)
+        w_scales = resident.tile([P, 2 * len(OPERANDS), H], U8, align_bytes=64)
+        w_nat = {}
+
+        def operand(side, name):
+            return side * len(OPERANDS) + OPERANDS.index(name)
+
+        def unit_span(unit):
+            return max(0, (unit - 1) * UNIT_BLOCKS + 1), unit * UNIT_BLOCKS + 1
+
+        def load_weight(side, chunk):
+            if chunk == "centre":
+                rows = centres[side]
+            else:
+                rows = gates[side][GATE_CHUNK[chunk] * H : (GATE_CHUNK[chunk] + 1) * H, :]
+            w_nat[(side, chunk)] = resident.tile([P, H // P, K], BF16, name="w_nat_%d_%s" % (side, chunk))
+            nc.sync.dma_start(out=w_nat[(side, chunk)][:], in_=rows.rearrange("(t p) k -> p t k", p=P))
+
+        def load_x(unit):
+            first, end = unit_span(unit)
+            nc.sync.dma_start(out=x_nat[:, first:end, :], in_=x_rows[:, first:end, :])
+
+        def load_mix(unit):
+            first, end = unit_span(unit)
+            nc.sync.dma_start(out=mix_in[:, first:end, :], in_=mix_rows[:, first:end, :])
+
+        for chunk in ("g1", "g0"):
+            for side in (LEFT, RIGHT):
+                load_weight(side, chunk)
+        load_x(0)
+        load_x(1)
+        for side in (LEFT, RIGHT):
+            load_weight(side, "centre")
+        load_mix(0)
+        load_mix(1)
+        load_x(2)
+        load_mix(2)
+        for side in (LEFT, RIGHT):
+            load_weight(side, "g2")
+        for unit in range(LEAD, UNITS):
+            load_x(unit)
+            load_mix(unit)
+
+        def transpose_words(nat):
+            tiles = nat.shape[1]
+            nat_words = nat.bitcast(F32)
+            words = psum.tile([P, 2, tiles * P], F32, tag="bank", bufs=PSUM_BANKS)
+            for u in range(2):
+                for t in range(tiles):
+                    nc.tensor.transpose(
+                        out=words[:, u, t * P : (t + 1) * P],
+                        in_=nat_words[:, t, u : 2 * P : 2],
+                        identity=ident_words[:],
+                    )
+            return words
+
+        def copy_words(copy, words, grouped):
+            copy(
+                out=grouped.bitcast(F32).rearrange("p (r u) -> p r u", u=2),
+                in_=words[:].rearrange("p u r -> p r u"),
+            )
+
+        def quantise(values, codes, scales):
+            nc.vector.quantize_mx(out=codes.bitcast(FP8X4), scales=scales, in_=values)
+
+        def prepare_weight(side, chunk):
+            words = transpose_words(w_nat[(side, chunk)][:])
+            grouped = stage.tile([P, 4 * H], BF16, tag="w_grouped", align_bytes=64)
+            copy_words(nc.scalar.copy if side == LEFT else nc.vector.tensor_copy, words, grouped[:])
+            plain, negated = CHUNK_USES[chunk]
+            if plain is not None:
+                w = operand(side, plain)
+                quantise(grouped[:], w_codes[:, w, :], w_scales[:, w, :])
+            if negated is not None:
+                w = operand(side, negated)
+                turned = stage.tile([P, 4 * H], BF16, tag="turned", align_bytes=64)
+                nc.vector.tensor_scalar_mul(out=turned[:], in0=grouped[:], scalar1=-1.0)
+                quantise(turned[:], w_codes[:, w, :], w_scales[:, w, :])
+
+        x_words, x_grouped = {}, {}
+
+        def unit_pieces(unit):
+            first, end = unit_span(unit)
+            return [(at, min(at + PIECE_BLOCKS, end)) for at in range(first, end, PIECE_BLOCKS)]
+
+        def transpose_unit(unit):
+            x_words[unit] = [transpose_words(x_nat[:, at:to, :]) for at, to in unit_pieces(unit)]
+
+        def copy_unit(unit):
+            first, end = unit_span(unit)
+            x_grouped[unit] = stage.tile([P, 4 * P * (end - first)], BF16, name="x_grouped", tag="x_grouped", align_bytes=64)
+            for (at, to), words in zip(unit_pieces(unit), x_words[unit]):
+                copy_words(nc.scalar.copy, words, x_grouped[unit][:, 4 * P * (at - first) : 4 * P * (to - first)])
+
+        def quantise_unit(unit):
+            first, end = unit_span(unit)
+            quantise(
+                x_grouped[unit][:],
+                x_codes[:, first:end, :].rearrange("p s r -> p (s r)"),
+                x_scales[:, first:end, :].rearrange("p s r -> p (s r)"),
+            )
+
+        def project(acc, block, names):
+            passes = [(block + side, operand(side, name)) for side in (LEFT, RIGHT) for name in names]
+            for n, (x_block, w) in enumerate(passes):
+                nc.tensor.matmul_mx(
+                    out=acc,
+                    lhsT=x_codes[:, x_block, :].bitcast(FP8X4),
+                    lhsT_scale=x_scales[:, x_block, :],
+                    rhs=w_codes[:, w, :].bitcast(FP8X4),
+                    rhs_scale=w_scales[:, w, :],
+                    start=(n == 0),
+                    stop=(n == len(passes) - 1),
+                )
+
+        def new_bank():
+            return psum.tile([P, PAIR_COLS], F32, name="bank", tag="bank", bufs=PSUM_BANKS)
+
+        def project_pair(pair, names):
+            bank = new_bank()
+            for half in range(2):
+                project(bank[:, half * H : (half + 1) * H], 2 * pair + half, names)
+            return bank
+
+        def mixed(first, count):
+            return mix_in[:, first : first + count, :].rearrange("p s h -> p (s h)")
+
+        def part(tiles, pair):
+            at = (pair % GROUP_PAIRS) * PAIR_COLS
+            return tiles[pair // GROUP_PAIRS][:, at : at + PAIR_COLS]
+
+        d_bank, c_bank, lr_bank = {}, {}, {}
+        centre = {}
+        share, logit, mix, diff = {}, {}, {}, {}
+
+        def open_group(group):
+            centre[group] = stage.tile([P, GROUP_COLS], F32, name="centre", tag="centre")
+            share[group] = keep.tile([P, GROUP_COLS], F32, name="share", tag="share")
+            logit[group] = keep.tile([P, GROUP_COLS], F32, name="logit", tag="logit")
+            mix[group] = keep.tile([P, GROUP_COLS], F32, name="mix", tag="mix")
+            diff[group] = keep.tile([P, GROUP_COLS], F32, name="diff", tag="diff")
+
+        def tensor_first(pair):
+            d_bank[pair] = project_pair(pair, ("g0", "neg_g1"))
+            c_bank[pair] = project_pair(pair, ("centre",))
+            lr_bank[pair] = new_bank()
+            nc.tensor.matmul(out=lr_bank[pair][:], lhsT=ident[:], rhs=mixed(2 * pair, 2), start=True, stop=False)
+            nc.tensor.matmul(out=lr_bank[pair][:], lhsT=neg_ident[:], rhs=mixed(2 * pair + 1, 2), start=False, stop=True)
+
+        def scalar_first(pair):
+            nc.scalar.activation(out=part(logit, pair), in_=d_bank[pair][:], func=AF.Relu, bias=plus_floor[:])
+            nc.scalar.activation(out=part(centre, pair), in_=c_bank[pair][:], func=AF.Sigmoid)
+            nc.scalar.activation(out=part(share, pair), in_=part(logit, pair), func=AF.Sigmoid, bias=minus_floor[:])
+
+        def weigh_left(pair):
+            nc.vector.tensor_tensor(out=part(mix, pair), in0=part(share, pair), in1=lr_bank[pair][:], op=ALU.mult)
+
+        def add_right(group):
+            right = mixed(group * GROUP_POSITIONS + 1, GROUP_POSITIONS)
+            nc.vector.tensor_tensor(out=mix[group][:], in0=mix[group][:], in1=right, op=ALU.add)
+
+        def subtract_mix(group):
+            nc.vector.tensor_tensor(out=diff[group][:], in0=centre[group][:], in1=mix[group][:], op=ALU.subtract)
+
+        def logarithm(group):
+            nc.scalar.activation(out=share[group][:], in_=share[group][:], func=AF.Ln)
+
+        def add_b(group):
+            for pair in range(group * GROUP_PAIRS, (group + 1) * GROUP_PAIRS):
+                b_bank = project_pair(pair, ("g1", "neg_g2"))
+                nc.vector.tensor_tensor(out=part(logit, pair), in0=part(logit, pair), in1=b_bank[:], op=ALU.add)
+
+        def subtract_log(group):
+            nc.vector.tensor_tensor(out=logit[group][:], in0=logit[group][:], in1=share[group][:], op=ALU.subtract)
+
+        def centre_weight(group):
+            nc.scalar.activation(out=share[group][:], in_=logit[group][:], func=AF.Sigmoid, scale=-1.0, bias=plus_floor[:])
+
+        def weigh_centre(group):
+            nc.vector.tensor_tensor(out=diff[group][:], in0=diff[group][:], in1=share[group][:], op=ALU.mult)
+
+        def finish(group):
+            nc.vector.tensor_tensor(out=diff[group][:], in0=diff[group][:], in1=mix[group][:], op=ALU.add)
+            first = group * GROUP_POSITIONS
+            nc.sync.dma_start(
+                out=out_rows[:, first : first + GROUP_POSITIONS, :],
+                in_=diff[group][:].rearrange("p (s h) -> p s h", s=GROUP_POSITIONS),
+            )
+
+        def one_behind(first, lead, follow):
+            for n in range(ROUND + 1):
+                if n < ROUND:
+                    lead(first + n)
+                if n >= 1:
+                    follow(first + n - 1)
+
+        for chunk in ("g1", "g0"):
+            for side in (LEFT, RIGHT):
+                prepare_weight(side, chunk)
+        transpose_unit(0)
+        copy_unit(0)
+        transpose_unit(1)
+        copy_unit(1)
+        quantise_unit(0)
+        quantise_unit(1)
+        for side in (LEFT, RIGHT):
+            prepare_weight(side, "centre")
+        transpose_unit(2)
+        copy_unit(2)
+        quantise_unit(2)
+
+        tensor_first(0)
+        for group in range(GROUPS):
+            old = group - ROUND
+            new_unit = group + LEAD
+            early, late = group * GROUP_PAIRS, group * GROUP_PAIRS + 1
+            open_group(group)
+            if new_unit < UNITS:
+                transpose_unit(new_unit)
+            tensor_first(late)
+            scalar_first(early)
+            weigh_left(early)
+            if new_unit < UNITS:
+                copy_unit(new_unit)
+            if late + 1 < PAIRS:
+                tensor_first(late + 1)
+            if old >= 0:
+                centre_weight(old)
+                weigh_centre(old)
+            scalar_first(late)
+            weigh_left(late)
+            add_right(group)
+            if new_unit < UNITS:
+                quantise_unit(new_unit)
+            if old >= 0:
+                finish(old)
+            subtract_mix(group)
+            if group in (LEFT, RIGHT):
+                prepare_weight(group, "g2")
+            if (group + 1) % ROUND == 0:
+                first = group + 1 - ROUND
+                for done in range(first, group + 1):
+                    logarithm(done)
+                one_behind(first, add_b, subtract_log)
+        for group in range(GROUPS - ROUND, GROUPS):
+            centre_weight(group)
+        one_behind(GROUPS - ROUND, weigh_centre, finish)

@@ -22,17 +22,21 @@ GROUP_PAIRS = 2
 GROUP_POSITIONS = 2 * GROUP_PAIRS
 GROUP_COLS = GROUP_PAIRS * PAIR_COLS
 GROUPS = PAIRS // GROUP_PAIRS
-ROUND = 4
+ROUND_PAIRS = 4
+ROUND_GROUPS = ROUND_PAIRS // GROUP_PAIRS
 PIECE_BLOCKS = 2
-UNIT_BLOCKS = GROUP_POSITIONS
-UNITS = GROUPS + 1
-LEAD = 3
+UNIT_BLOCKS = (1, 2, 2, 4, 4, 4, 4, 4, 4, 4)
+UNIT_FIRST = tuple(sum(UNIT_BLOCKS[:u]) for u in range(len(UNIT_BLOCKS)))
+UNITS = len(UNIT_BLOCKS)
+HEAD_UNITS = 4
+VECTOR_GROUPS = 3
 FLOOR = 40.0
 PSUM_BANKS = 8
 
 LEFT, RIGHT = 0, 1
-OPERANDS = ("centre", "g0", "g1", "neg_g1", "neg_g2")
-CHUNK_USES = {"centre": ("centre", None), "g0": ("g0", None), "g1": ("g1", "neg_g1"), "g2": (None, "neg_g2")}
+SIDES = (LEFT, RIGHT)
+OPERANDS = ("centre", "g0", "neg_g1", "g2")
+CHUNKS = ("centre", "g0", "g1", "g2")
 GATE_CHUNK = {"g0": 0, "g1": 1, "g2": 2}
 
 FLOPS = 2 * POSITIONS * P * (2 * K) * (4 * H)
@@ -51,8 +55,8 @@ def tile_grconv_pa_t_kernel(tc, x, x_mix, WL, WR, GL, GR, out):
         const = ctx.enter_context(tc.tile_pool(name="const", bufs=1))
         resident = ctx.enter_context(tc.tile_pool(name="resident", bufs=1))
         stage = ctx.enter_context(tc.tile_pool(name="stage", bufs=3))
-        keep = ctx.enter_context(tc.tile_pool(name="keep", bufs=ROUND + 1))
-        psum = ctx.enter_context(tc.psum_pool(name="psum", bufs=1))
+        keep = ctx.enter_context(tc.tile_pool(name="keep", bufs=2 * ROUND_GROUPS + 1))
+        psum = ctx.enter_context(tc.psum_pool(name="psum", bufs=PSUM_BANKS))
 
         plus_floor = const.tile([P, 1], F32)
         nc.vector.memset(plus_floor[:], FLOOR)
@@ -79,7 +83,7 @@ def tile_grconv_pa_t_kernel(tc, x, x_mix, WL, WR, GL, GR, out):
             return side * len(OPERANDS) + OPERANDS.index(name)
 
         def unit_span(unit):
-            return max(0, (unit - 1) * UNIT_BLOCKS + 1), unit * UNIT_BLOCKS + 1
+            return UNIT_FIRST[unit], UNIT_FIRST[unit] + UNIT_BLOCKS[unit]
 
         def load_weight(side, chunk):
             if chunk == "centre":
@@ -97,27 +101,30 @@ def tile_grconv_pa_t_kernel(tc, x, x_mix, WL, WR, GL, GR, out):
             first, end = unit_span(unit)
             nc.sync.dma_start(out=mix_in[:, first:end, :], in_=mix_rows[:, first:end, :])
 
-        for chunk in ("g1", "g0"):
-            for side in (LEFT, RIGHT):
-                load_weight(side, chunk)
+        for side in SIDES:
+            load_weight(side, "g1")
         load_x(0)
         load_x(1)
-        for side in (LEFT, RIGHT):
-            load_weight(side, "centre")
-        load_mix(0)
-        load_mix(1)
+        for side in SIDES:
+            load_weight(side, "g0")
+        for unit in range(3):
+            load_mix(unit)
         load_x(2)
-        load_mix(2)
-        for side in (LEFT, RIGHT):
+        for side in SIDES:
+            load_weight(side, "centre")
+        for unit in (3, 4):
+            load_x(unit)
+            load_mix(unit)
+        for side in SIDES:
             load_weight(side, "g2")
-        for unit in range(LEAD, UNITS):
+        for unit in range(5, UNITS):
             load_x(unit)
             load_mix(unit)
 
         def transpose_words(nat):
             tiles = nat.shape[1]
             nat_words = nat.bitcast(F32)
-            words = psum.tile([P, 2, tiles * P], F32, tag="bank", bufs=PSUM_BANKS)
+            words = psum.tile([P, 2, tiles * P], F32, tag="bank")
             for u in range(2):
                 for t in range(tiles):
                     nc.tensor.transpose(
@@ -136,19 +143,24 @@ def tile_grconv_pa_t_kernel(tc, x, x_mix, WL, WR, GL, GR, out):
         def quantise(values, codes, scales):
             nc.vector.quantize_mx(out=codes.bitcast(FP8X4), scales=scales, in_=values)
 
-        def prepare_weight(side, chunk):
-            words = transpose_words(w_nat[(side, chunk)][:])
-            grouped = stage.tile([P, 4 * H], BF16, tag="w_grouped", align_bytes=64)
-            copy_words(nc.scalar.copy if side == LEFT else nc.vector.tensor_copy, words, grouped[:])
-            plain, negated = CHUNK_USES[chunk]
-            if plain is not None:
-                w = operand(side, plain)
-                quantise(grouped[:], w_codes[:, w, :], w_scales[:, w, :])
-            if negated is not None:
-                w = operand(side, negated)
-                turned = stage.tile([P, 4 * H], BF16, tag="turned", align_bytes=64)
-                nc.vector.tensor_scalar_mul(out=turned[:], in0=grouped[:], scalar1=-1.0)
-                quantise(turned[:], w_codes[:, w, :], w_scales[:, w, :])
+        w_words, w_grouped = {}, {}
+
+        def transpose_weight(side, chunk):
+            w_words[(side, chunk)] = transpose_words(w_nat[(side, chunk)][:])
+
+        def copy_weight(copy, side, chunk):
+            grouped = stage.tile([P, 4 * H], BF16, name="grouped", tag="w_grouped", align_bytes=64)
+            copy_words(copy, w_words[(side, chunk)], grouped[:])
+            w_grouped[(side, chunk)] = grouped
+
+        def turn_weight(side, chunk):
+            turned = stage.tile([P, 4 * H], BF16, name="turned", tag="w_turned", align_bytes=64)
+            nc.vector.tensor_scalar_mul(out=turned[:], in0=w_grouped[(side, chunk)][:], scalar1=-1.0)
+            w_grouped[(side, chunk)] = turned
+
+        def quantise_weight(side, chunk):
+            w = operand(side, OPERANDS[CHUNKS.index(chunk)])
+            quantise(w_grouped[(side, chunk)][:], w_codes[:, w, :], w_scales[:, w, :])
 
         x_words, x_grouped = {}, {}
 
@@ -174,7 +186,7 @@ def tile_grconv_pa_t_kernel(tc, x, x_mix, WL, WR, GL, GR, out):
             )
 
         def project(acc, block, names):
-            passes = [(block + side, operand(side, name)) for side in (LEFT, RIGHT) for name in names]
+            passes = [(block + side, operand(side, name)) for side in SIDES for name in names]
             for n, (x_block, w) in enumerate(passes):
                 nc.tensor.matmul_mx(
                     out=acc,
@@ -187,7 +199,7 @@ def tile_grconv_pa_t_kernel(tc, x, x_mix, WL, WR, GL, GR, out):
                 )
 
         def new_bank():
-            return psum.tile([P, PAIR_COLS], F32, name="bank", tag="bank", bufs=PSUM_BANKS)
+            return psum.tile([P, PAIR_COLS], F32, name="bank", tag="bank")
 
         def project_pair(pair, names):
             bank = new_bank()
@@ -202,119 +214,174 @@ def tile_grconv_pa_t_kernel(tc, x, x_mix, WL, WR, GL, GR, out):
             at = (pair % GROUP_PAIRS) * PAIR_COLS
             return tiles[pair // GROUP_PAIRS][:, at : at + PAIR_COLS]
 
-        d_bank, c_bank, lr_bank = {}, {}, {}
-        centre = {}
-        share, logit, mix, diff = {}, {}, {}, {}
+        d_bank, c_bank, e_bank, gap = {}, {}, {}, {}
+        gap_tile = {}
+        centre, share, logit, mix, weight = {}, {}, {}, {}, {}
 
         def open_group(group):
-            centre[group] = stage.tile([P, GROUP_COLS], F32, name="centre", tag="centre")
-            share[group] = keep.tile([P, GROUP_COLS], F32, name="share", tag="share")
-            logit[group] = keep.tile([P, GROUP_COLS], F32, name="logit", tag="logit")
-            mix[group] = keep.tile([P, GROUP_COLS], F32, name="mix", tag="mix")
-            diff[group] = keep.tile([P, GROUP_COLS], F32, name="diff", tag="diff")
+            for tiles, pool, name in (
+                (share, stage, "share"),
+                (centre, keep, "centre"),
+                (logit, keep, "logit"),
+                (mix, keep, "mix"),
+                (weight, keep, "weight"),
+            ):
+                tiles[group] = pool.tile([P, GROUP_COLS], F32, name=name, tag=name)
 
-        def tensor_first(pair):
-            d_bank[pair] = project_pair(pair, ("g0", "neg_g1"))
-            c_bank[pair] = project_pair(pair, ("centre",))
-            lr_bank[pair] = new_bank()
-            nc.tensor.matmul(out=lr_bank[pair][:], lhsT=ident[:], rhs=mixed(2 * pair, 2), start=True, stop=False)
-            nc.tensor.matmul(out=lr_bank[pair][:], lhsT=neg_ident[:], rhs=mixed(2 * pair + 1, 2), start=False, stop=True)
+        def gap_by_vector(group):
+            first = group * GROUP_POSITIONS
+            gap_tile[group] = stage.tile([P, GROUP_COLS], F32, name="gap", tag="gap")
+            nc.vector.tensor_tensor(
+                out=gap_tile[group][:],
+                in0=mixed(first, GROUP_POSITIONS),
+                in1=mixed(first + 1, GROUP_POSITIONS),
+                op=ALU.subtract,
+            )
+            for pair in range(group * GROUP_PAIRS, (group + 1) * GROUP_PAIRS):
+                gap[pair] = part(gap_tile, pair)
 
-        def scalar_first(pair):
+        def gap_by_tensor(pair):
+            bank = new_bank()
+            nc.tensor.matmul(out=bank[:], lhsT=ident[:], rhs=mixed(2 * pair, 2), start=True, stop=False)
+            nc.tensor.matmul(out=bank[:], lhsT=neg_ident[:], rhs=mixed(2 * pair + 1, 2), start=False, stop=True)
+            gap[pair] = bank[:]
+
+        def hold_d(pair):
             nc.scalar.activation(out=part(logit, pair), in_=d_bank[pair][:], func=AF.Relu, bias=plus_floor[:])
-            nc.scalar.activation(out=part(centre, pair), in_=c_bank[pair][:], func=AF.Sigmoid)
+
+        def split_sides(pair):
             nc.scalar.activation(out=part(share, pair), in_=part(logit, pair), func=AF.Sigmoid, bias=minus_floor[:])
 
+        def squash_centre(pair):
+            nc.scalar.activation(out=part(centre, pair), in_=c_bank[pair][:], func=AF.Sigmoid)
+
         def weigh_left(pair):
-            nc.vector.tensor_tensor(out=part(mix, pair), in0=part(share, pair), in1=lr_bank[pair][:], op=ALU.mult)
+            nc.vector.tensor_tensor(out=part(mix, pair), in0=part(share, pair), in1=gap[pair], op=ALU.mult)
 
         def add_right(group):
             right = mixed(group * GROUP_POSITIONS + 1, GROUP_POSITIONS)
             nc.vector.tensor_tensor(out=mix[group][:], in0=mix[group][:], in1=right, op=ALU.add)
 
         def subtract_mix(group):
-            nc.vector.tensor_tensor(out=diff[group][:], in0=centre[group][:], in1=mix[group][:], op=ALU.subtract)
+            nc.vector.tensor_tensor(out=centre[group][:], in0=centre[group][:], in1=mix[group][:], op=ALU.subtract)
 
         def logarithm(group):
-            nc.scalar.activation(out=share[group][:], in_=share[group][:], func=AF.Ln)
+            nc.scalar.activation(out=weight[group][:], in_=share[group][:], func=AF.Ln)
 
-        def add_b(group):
-            for pair in range(group * GROUP_PAIRS, (group + 1) * GROUP_PAIRS):
-                b_bank = project_pair(pair, ("g1", "neg_g2"))
-                nc.vector.tensor_tensor(out=part(logit, pair), in0=part(logit, pair), in1=b_bank[:], op=ALU.add)
+        def subtract_e(pair):
+            nc.vector.tensor_tensor(out=part(logit, pair), in0=part(logit, pair), in1=e_bank[pair][:], op=ALU.subtract)
 
         def subtract_log(group):
-            nc.vector.tensor_tensor(out=logit[group][:], in0=logit[group][:], in1=share[group][:], op=ALU.subtract)
+            nc.vector.tensor_tensor(out=logit[group][:], in0=logit[group][:], in1=weight[group][:], op=ALU.subtract)
 
         def centre_weight(group):
-            nc.scalar.activation(out=share[group][:], in_=logit[group][:], func=AF.Sigmoid, scale=-1.0, bias=plus_floor[:])
+            nc.scalar.activation(out=weight[group][:], in_=logit[group][:], func=AF.Sigmoid, scale=-1.0, bias=plus_floor[:])
 
         def weigh_centre(group):
-            nc.vector.tensor_tensor(out=diff[group][:], in0=diff[group][:], in1=share[group][:], op=ALU.mult)
+            nc.vector.tensor_tensor(out=centre[group][:], in0=centre[group][:], in1=weight[group][:], op=ALU.mult)
 
         def finish(group):
-            nc.vector.tensor_tensor(out=diff[group][:], in0=diff[group][:], in1=mix[group][:], op=ALU.add)
+            nc.vector.tensor_tensor(out=centre[group][:], in0=centre[group][:], in1=mix[group][:], op=ALU.add)
             first = group * GROUP_POSITIONS
             nc.sync.dma_start(
                 out=out_rows[:, first : first + GROUP_POSITIONS, :],
-                in_=diff[group][:].rearrange("p (s h) -> p s h", s=GROUP_POSITIONS),
+                in_=centre[group][:].rearrange("p (s h) -> p s h", s=GROUP_POSITIONS),
             )
 
-        def one_behind(first, lead, follow):
-            for n in range(ROUND + 1):
-                if n < ROUND:
-                    lead(first + n)
-                if n >= 1:
-                    follow(first + n - 1)
-
-        for chunk in ("g1", "g0"):
-            for side in (LEFT, RIGHT):
-                prepare_weight(side, chunk)
-        transpose_unit(0)
-        copy_unit(0)
-        transpose_unit(1)
-        copy_unit(1)
-        quantise_unit(0)
-        quantise_unit(1)
-        for side in (LEFT, RIGHT):
-            prepare_weight(side, "centre")
+        for side, copy in zip(SIDES, (nc.scalar.copy, nc.vector.tensor_copy)):
+            transpose_weight(side, "g1")
+            copy_weight(copy, side, "g1")
+            turn_weight(side, "g1")
+            quantise_weight(side, "g1")
+        for unit in range(2):
+            transpose_unit(unit)
+            copy_unit(unit)
+            quantise_unit(unit)
+        for side, copy in zip(SIDES, (nc.scalar.copy, nc.vector.tensor_copy)):
+            transpose_weight(side, "g0")
+            copy_weight(copy, side, "g0")
+            quantise_weight(side, "g0")
         transpose_unit(2)
         copy_unit(2)
         quantise_unit(2)
+        for side in SIDES:
+            transpose_weight(side, "centre")
+            copy_weight(nc.scalar.copy, side, "centre")
+        transpose_unit(3)
+        copy_unit(3)
+        for group in range(VECTOR_GROUPS):
+            gap_by_vector(group)
+        for side in SIDES:
+            quantise_weight(side, "centre")
+        quantise_unit(3)
 
-        tensor_first(0)
-        for group in range(GROUPS):
-            old = group - ROUND
-            new_unit = group + LEAD
-            early, late = group * GROUP_PAIRS, group * GROUP_PAIRS + 1
-            open_group(group)
-            if new_unit < UNITS:
-                transpose_unit(new_unit)
-            tensor_first(late)
-            scalar_first(early)
-            weigh_left(early)
-            if new_unit < UNITS:
-                copy_unit(new_unit)
-            if late + 1 < PAIRS:
-                tensor_first(late + 1)
-            if old >= 0:
-                centre_weight(old)
-                weigh_centre(old)
-            scalar_first(late)
-            weigh_left(late)
-            add_right(group)
-            if new_unit < UNITS:
-                quantise_unit(new_unit)
-            if old >= 0:
-                finish(old)
-            subtract_mix(group)
-            if group in (LEFT, RIGHT):
-                prepare_weight(group, "g2")
-            if (group + 1) % ROUND == 0:
-                first = group + 1 - ROUND
-                for done in range(first, group + 1):
-                    logarithm(done)
-                one_behind(first, add_b, subtract_log)
-        for group in range(GROUPS - ROUND, GROUPS):
-            centre_weight(group)
-        one_behind(GROUPS - ROUND, weigh_centre, finish)
+        for n in range(PAIRS + 2):
+            phase = n % ROUND_PAIRS
+            round_pairs = range(n - phase - ROUND_PAIRS, n - phase) if n >= ROUND_PAIRS else range(0)
+            round_groups = [pair // GROUP_PAIRS for pair in round_pairs[::GROUP_PAIRS]]
+            unit = HEAD_UNITS + n // 2
+            new_unit = n % 2 == 1 and unit < UNITS
+            if n < PAIRS:
+                if n % GROUP_PAIRS == 0:
+                    open_group(n // GROUP_PAIRS)
+                if new_unit:
+                    transpose_unit(unit)
+                    copy_unit(unit)
+                d_bank[n] = project_pair(n, ("g0", "neg_g1"))
+                hold_d(n)
+            if n == 1:
+                for side in SIDES:
+                    transpose_weight(side, "g2")
+                    copy_weight(nc.scalar.copy, side, "g2")
+            if phase == 0:
+                for group in round_groups:
+                    logarithm(group)
+                for pair in round_pairs[:1]:
+                    e_bank[pair] = project_pair(pair, ("g2", "neg_g1"))
+            if 2 <= n < PAIRS + 2:
+                c_bank[n - 2] = project_pair(n - 2, ("centre",))
+                squash_centre(n - 2)
+            if phase == 0:
+                for pair in round_pairs[1:]:
+                    e_bank[pair] = project_pair(pair, ("g2", "neg_g1"))
+            if n < PAIRS:
+                split_sides(n)
+            if phase == 1:
+                for group in round_groups:
+                    centre_weight(group)
+            if 1 <= n <= PAIRS:
+                pair = n - 1
+                group = pair // GROUP_PAIRS
+                if group >= VECTOR_GROUPS:
+                    gap_by_tensor(pair)
+                weigh_left(pair)
+                if n == 2:
+                    for side in SIDES:
+                        quantise_weight(side, "g2")
+                if phase == 1:
+                    if new_unit:
+                        quantise_unit(unit)
+                    if group > 0:
+                        subtract_mix(group - 1)
+                elif phase == 2:
+                    for old in round_groups:
+                        weigh_centre(old)
+                    add_right(group)
+                elif phase == 3:
+                    if new_unit:
+                        quantise_unit(unit)
+                    for old in round_groups:
+                        finish(old)
+                    subtract_mix(group - 1)
+                else:
+                    for old in round_pairs:
+                        subtract_e(old)
+                    add_right(group)
+                    for old in round_groups:
+                        subtract_log(old)
+        last = range(GROUPS - ROUND_GROUPS, GROUPS)
+        subtract_mix(GROUPS - 1)
+        for group in last:
+            weigh_centre(group)
+        for group in last:
+            finish(group)

@@ -22,8 +22,31 @@ GROUP_PAIRS = 2
 GROUP_POSITIONS = 2 * GROUP_PAIRS
 GROUP_COLS = GROUP_PAIRS * PAIR_COLS
 GROUPS = PAIRS // GROUP_PAIRS
-ROUND_PAIRS = 4
-ROUND_GROUPS = ROUND_PAIRS // GROUP_PAIRS
+ROUNDS = (2, 2, 2, 2)
+EP = 4
+EPL = 4
+KEEP = 5
+WARM = 5
+LATEC = False
+GAPB = 3
+WB = 4
+SHB = 3
+XB = 3
+FINE = {6: 2, 7: 2}
+GPC = 4
+DVG = 0
+SMG = ()
+XV = [(2, u) for u in range(4, 10)]
+GV = (("c", 1),)
+LNPOS = 1
+CL = 2
+QK = 1
+WK = 2
+FK = 3
+G2N = 1
+EFIRST = 0
+ADDR = 1
+G0A = True
 PIECE_BLOCKS = 2
 UNIT_BLOCKS = (1, 2, 2, 4, 4, 4, 4, 4, 4, 4)
 UNIT_FIRST = tuple(sum(UNIT_BLOCKS[:u]) for u in range(len(UNIT_BLOCKS)))
@@ -54,10 +77,16 @@ def tile_grconv_pa_t_kernel(tc, x, x_mix, WL, WR, GL, GR, out):
         ctx.enter_context(tc.manual_schedule())
         const = ctx.enter_context(tc.tile_pool(name="const", bufs=1))
         resident = ctx.enter_context(tc.tile_pool(name="resident", bufs=1))
-        stage = ctx.enter_context(tc.tile_pool(name="stage", bufs=3))
-        keep = ctx.enter_context(tc.tile_pool(name="keep", bufs=2 * ROUND_GROUPS + 1))
+        stage = ctx.enter_context(tc.tile_pool(name="stage", bufs=2))
+        gapp = ctx.enter_context(tc.tile_pool(name="gapp", bufs=GAPB))
+        wp = ctx.enter_context(tc.tile_pool(name="wp", bufs=4))
+        weightp = ctx.enter_context(tc.tile_pool(name="weightp", bufs=WB))
+        sharep = ctx.enter_context(tc.tile_pool(name="sharep", bufs=SHB))
+        keep = ctx.enter_context(tc.tile_pool(name="keep", bufs=KEEP))
         psum = ctx.enter_context(tc.psum_pool(name="psum", bufs=PSUM_BANKS))
 
+        zeros = const.tile([P, PAIR_COLS], BF16)
+        nc.vector.memset(zeros[:], 0.0)
         plus_floor = const.tile([P, 1], F32)
         nc.vector.memset(plus_floor[:], FLOOR)
         minus_floor = const.tile([P, 1], F32)
@@ -69,7 +98,6 @@ def tile_grconv_pa_t_kernel(tc, x, x_mix, WL, WR, GL, GR, out):
         ident = const.tile([P, P], BF16)
         make_identity(nc, ident[:])
         neg_ident = const.tile([P, P], BF16)
-        nc.vector.tensor_scalar_mul(out=neg_ident[:], in0=ident[:], scalar1=-1.0)
 
         x_nat = resident.tile([P, BLOCKS, K], BF16)
         mix_in = resident.tile([P, BLOCKS, H], BF16)
@@ -101,22 +129,23 @@ def tile_grconv_pa_t_kernel(tc, x, x_mix, WL, WR, GL, GR, out):
             first, end = unit_span(unit)
             nc.sync.dma_start(out=mix_in[:, first:end, :], in_=mix_rows[:, first:end, :])
 
-        for side in SIDES:
-            load_weight(side, "g1")
+        load_weight(LEFT, "g1")
         load_x(0)
         load_x(1)
+        load_weight(RIGHT, "g1")
         for side in SIDES:
             load_weight(side, "g0")
+        load_x(2)
         for unit in range(3):
             load_mix(unit)
-        load_x(2)
+        load_x(3)
         for side in SIDES:
             load_weight(side, "centre")
-        for unit in (3, 4):
-            load_x(unit)
-            load_mix(unit)
+        load_x(4)
+        load_mix(3)
         for side in SIDES:
             load_weight(side, "g2")
+        load_mix(4)
         for unit in range(5, UNITS):
             load_x(unit)
             load_mix(unit)
@@ -149,14 +178,13 @@ def tile_grconv_pa_t_kernel(tc, x, x_mix, WL, WR, GL, GR, out):
             w_words[(side, chunk)] = transpose_words(w_nat[(side, chunk)][:])
 
         def copy_weight(copy, side, chunk):
-            grouped = stage.tile([P, 4 * H], BF16, name="grouped", tag="w_grouped", align_bytes=64)
+            grouped = wp.tile([P, 4 * H], BF16, name="grouped", tag="w_grouped", align_bytes=64)
             copy_words(copy, w_words[(side, chunk)], grouped[:])
             w_grouped[(side, chunk)] = grouped
 
         def turn_weight(side, chunk):
-            turned = stage.tile([P, 4 * H], BF16, name="turned", tag="w_turned", align_bytes=64)
-            nc.vector.tensor_scalar_mul(out=turned[:], in0=w_grouped[(side, chunk)][:], scalar1=-1.0)
-            w_grouped[(side, chunk)] = turned
+            nat = w_nat[(side, chunk)][:].rearrange("p t k -> p (t k)")
+            nc.vector.tensor_scalar_mul(out=nat, in0=nat, scalar1=-1.0)
 
         def quantise_weight(side, chunk):
             w = operand(side, OPERANDS[CHUNKS.index(chunk)])
@@ -173,9 +201,9 @@ def tile_grconv_pa_t_kernel(tc, x, x_mix, WL, WR, GL, GR, out):
 
         def copy_unit(unit):
             first, end = unit_span(unit)
-            x_grouped[unit] = stage.tile([P, 4 * P * (end - first)], BF16, name="x_grouped", tag="x_grouped", align_bytes=64)
+            x_grouped[unit] = stage.tile([P, 4 * P * (end - first)], BF16, name="x_grouped", tag="x_grouped", align_bytes=64, bufs=XB)
             for (at, to), words in zip(unit_pieces(unit), x_words[unit]):
-                copy_words(nc.scalar.copy, words, x_grouped[unit][:, 4 * P * (at - first) : 4 * P * (to - first)])
+                copy_words(nc.vector.tensor_copy if unit in XV or (at - first, unit) in XV else nc.scalar.copy, words, x_grouped[unit][:, 4 * P * (at - first) : 4 * P * (to - first)])
 
         def quantise_unit(unit):
             first, end = unit_span(unit)
@@ -220,23 +248,23 @@ def tile_grconv_pa_t_kernel(tc, x, x_mix, WL, WR, GL, GR, out):
 
         def open_group(group):
             for tiles, pool, name in (
-                (share, stage, "share"),
+                (share, sharep, "share"),
                 (centre, keep, "centre"),
                 (logit, keep, "logit"),
                 (mix, keep, "mix"),
-                (weight, keep, "weight"),
             ):
                 tiles[group] = pool.tile([P, GROUP_COLS], F32, name=name, tag=name)
 
         def gap_by_vector(group):
             first = group * GROUP_POSITIONS
-            gap_tile[group] = stage.tile([P, GROUP_COLS], F32, name="gap", tag="gap")
-            nc.vector.tensor_tensor(
-                out=gap_tile[group][:],
-                in0=mixed(first, GROUP_POSITIONS),
-                in1=mixed(first + 1, GROUP_POSITIONS),
-                op=ALU.subtract,
-            )
+            gap_tile[group] = gapp.tile([P, GROUP_COLS], F32, name="gap", tag="gap")
+            for s in range(0, GROUP_POSITIONS, GPC):
+                (nc.gpsimd if DVG else nc.vector).tensor_tensor(
+                    out=gap_tile[group][:, s * H : (s + GPC) * H],
+                    in0=mixed(first + s, GPC),
+                    in1=mixed(first + s + 1, GPC),
+                    op=ALU.subtract,
+                )
             for pair in range(group * GROUP_PAIRS, (group + 1) * GROUP_PAIRS):
                 gap[pair] = part(gap_tile, pair)
 
@@ -245,6 +273,10 @@ def tile_grconv_pa_t_kernel(tc, x, x_mix, WL, WR, GL, GR, out):
             nc.tensor.matmul(out=bank[:], lhsT=ident[:], rhs=mixed(2 * pair, 2), start=True, stop=False)
             nc.tensor.matmul(out=bank[:], lhsT=neg_ident[:], rhs=mixed(2 * pair + 1, 2), start=False, stop=True)
             gap[pair] = bank[:]
+
+        def cuts(group):
+            n = FINE.get(group, 1)
+            return [slice(i * GROUP_COLS // n, (i + 1) * GROUP_COLS // n) for i in range(n)]
 
         def hold_d(pair):
             nc.scalar.activation(out=part(logit, pair), in_=d_bank[pair][:], func=AF.Relu, bias=plus_floor[:])
@@ -263,125 +295,161 @@ def tile_grconv_pa_t_kernel(tc, x, x_mix, WL, WR, GL, GR, out):
             nc.vector.tensor_tensor(out=mix[group][:], in0=mix[group][:], in1=right, op=ALU.add)
 
         def subtract_mix(group):
-            nc.vector.tensor_tensor(out=centre[group][:], in0=centre[group][:], in1=mix[group][:], op=ALU.subtract)
+            if group in SMG:
+                for pair in range(group * GROUP_PAIRS, (group + 1) * GROUP_PAIRS):
+                    nc.gpsimd.tensor_tensor(out=part(centre, pair), in0=part(centre, pair), in1=part(mix, pair), op=ALU.subtract)
+            else:
+                nc.vector.tensor_tensor(out=centre[group][:], in0=centre[group][:], in1=mix[group][:], op=ALU.subtract)
 
         def logarithm(group):
-            nc.scalar.activation(out=weight[group][:], in_=share[group][:], func=AF.Ln)
+            weight[group] = weightp.tile([P, GROUP_COLS], F32, name="weight", tag="weight")
+            for sl in cuts(group):
+                nc.scalar.activation(out=weight[group][:, sl], in_=share[group][:, sl], func=AF.Ln)
 
         def subtract_e(pair):
             nc.vector.tensor_tensor(out=part(logit, pair), in0=part(logit, pair), in1=e_bank[pair][:], op=ALU.subtract)
 
         def subtract_log(group):
-            nc.vector.tensor_tensor(out=logit[group][:], in0=logit[group][:], in1=weight[group][:], op=ALU.subtract)
+            for sl in cuts(group):
+                nc.vector.tensor_tensor(out=logit[group][:, sl], in0=logit[group][:, sl], in1=weight[group][:, sl], op=ALU.subtract)
 
         def centre_weight(group):
-            nc.scalar.activation(out=weight[group][:], in_=logit[group][:], func=AF.Sigmoid, scale=-1.0, bias=plus_floor[:])
+            for sl in cuts(group):
+                nc.scalar.activation(out=weight[group][:, sl], in_=logit[group][:, sl], func=AF.Sigmoid, scale=-1.0, bias=plus_floor[:])
 
         def weigh_centre(group):
-            nc.vector.tensor_tensor(out=centre[group][:], in0=centre[group][:], in1=weight[group][:], op=ALU.mult)
+            for sl in cuts(group):
+                nc.vector.tensor_tensor(out=centre[group][:, sl], in0=centre[group][:, sl], in1=weight[group][:, sl], op=ALU.mult)
 
         def finish(group):
-            nc.vector.tensor_tensor(out=centre[group][:], in0=centre[group][:], in1=mix[group][:], op=ALU.add)
             first = group * GROUP_POSITIONS
-            nc.sync.dma_start(
-                out=out_rows[:, first : first + GROUP_POSITIONS, :],
-                in_=centre[group][:].rearrange("p (s h) -> p s h", s=GROUP_POSITIONS),
-            )
+            for i, sl in enumerate(cuts(group)):
+                nc.vector.tensor_tensor(out=centre[group][:, sl], in0=centre[group][:, sl], in1=mix[group][:, sl], op=ALU.add)
+                w = GROUP_POSITIONS // len(cuts(group))
+                nc.sync.dma_start(
+                    out=out_rows[:, first + i * w : first + (i + 1) * w, :],
+                    in_=centre[group][:, sl].rearrange("p (s h) -> p s h", s=w),
+                )
 
-        for side, copy in zip(SIDES, (nc.scalar.copy, nc.vector.tensor_copy)):
-            transpose_weight(side, "g1")
-            copy_weight(copy, side, "g1")
-            turn_weight(side, "g1")
-            quantise_weight(side, "g1")
+        if WARM:
+            bank = new_bank()
+            for n in range(WARM):
+                nc.tensor.matmul(out=bank[:], lhsT=zeros[:, :P], rhs=zeros[:], start=True, stop=True)
         for unit in range(2):
             transpose_unit(unit)
             copy_unit(unit)
-            quantise_unit(unit)
-        for side, copy in zip(SIDES, (nc.scalar.copy, nc.vector.tensor_copy)):
+        turn_weight(LEFT, "g1")
+        turn_weight(RIGHT, "g1")
+        nc.vector.tensor_scalar_mul(out=neg_ident[:], in0=ident[:], scalar1=-1.0)
+        for side in SIDES:
+            transpose_weight(side, "g1")
+        copy_weight(nc.scalar.copy, LEFT, "g1")
+        quantise_unit(0)
+        quantise_unit(1)
+        copy_weight(nc.vector.tensor_copy, RIGHT, "g1")
+        for side in SIDES:
             transpose_weight(side, "g0")
-            copy_weight(copy, side, "g0")
+            copy_weight(nc.scalar.copy if side == LEFT or G0A else nc.vector.tensor_copy, side, "g0")
+        for side in SIDES:
+            quantise_weight(side, "g1")
+        for side in SIDES:
             quantise_weight(side, "g0")
         transpose_unit(2)
         copy_unit(2)
         quantise_unit(2)
-        for side in SIDES:
-            transpose_weight(side, "centre")
-            copy_weight(nc.scalar.copy, side, "centre")
         transpose_unit(3)
         copy_unit(3)
+        if not LATEC:
+            for side in SIDES:
+                transpose_weight(side, "centre")
+                copy_weight(nc.vector.tensor_copy if ("c", side) in GV else nc.scalar.copy, side, "centre")
         for group in range(VECTOR_GROUPS):
             gap_by_vector(group)
-        for side in SIDES:
-            quantise_weight(side, "centre")
         quantise_unit(3)
+        if not LATEC:
+            for side in SIDES:
+                quantise_weight(side, "centre")
 
-        for n in range(PAIRS + 2):
-            phase = n % ROUND_PAIRS
-            round_pairs = range(n - phase - ROUND_PAIRS, n - phase) if n >= ROUND_PAIRS else range(0)
-            round_groups = [pair // GROUP_PAIRS for pair in round_pairs[::GROUP_PAIRS]]
+        ends = {}
+        first = 0
+        for size in ROUNDS:
+            ends[(first + size) * GROUP_PAIRS] = list(range(first, first + size))
+            first += size
+
+        def at(step, lag):
+            return ends.get(step - lag, [])
+
+        def e_pairs(step):
+            for end in ends:
+                k = step - end
+                per = EP if end < PAIRS else EPL
+                pairs = range(ends[end][0] * GROUP_PAIRS, end)
+                if 0 <= k and k * per < len(pairs):
+                    return list(pairs[k * per : (k + 1) * per])
+            return []
+
+        for n in range(PAIRS + 8):
             unit = HEAD_UNITS + n // 2
             new_unit = n % 2 == 1 and unit < UNITS
+            es = e_pairs(n)
             if n < PAIRS:
                 if n % GROUP_PAIRS == 0:
                     open_group(n // GROUP_PAIRS)
                 if new_unit:
                     transpose_unit(unit)
                     copy_unit(unit)
+                if n == 1 and LATEC:
+                    for side in SIDES:
+                        transpose_weight(side, "centre")
+                        copy_weight(nc.vector.tensor_copy if ("c", side) in GV else nc.scalar.copy, side, "centre")
                 d_bank[n] = project_pair(n, ("g0", "neg_g1"))
                 hold_d(n)
-            if n == 1:
+            if n == G2N:
                 for side in SIDES:
                     transpose_weight(side, "g2")
-                    copy_weight(nc.scalar.copy, side, "g2")
-            if phase == 0:
-                for group in round_groups:
+                    copy_weight(nc.vector.tensor_copy if ("g2", side) in GV else nc.scalar.copy, side, "g2")
+            if LNPOS == 0:
+                for group in at(n, 0):
                     logarithm(group)
-                for pair in round_pairs[:1]:
-                    e_bank[pair] = project_pair(pair, ("g2", "neg_g1"))
-            if 2 <= n < PAIRS + 2:
-                c_bank[n - 2] = project_pair(n - 2, ("centre",))
-                squash_centre(n - 2)
-            if phase == 0:
-                for pair in round_pairs[1:]:
-                    e_bank[pair] = project_pair(pair, ("g2", "neg_g1"))
+            for pair in es[:EFIRST]:
+                e_bank[pair] = project_pair(pair, ("g2", "neg_g1"))
+            if CL <= n < PAIRS + CL:
+                c_bank[n - CL] = project_pair(n - CL, ("centre",))
+                squash_centre(n - CL)
+            for pair in es[EFIRST:]:
+                e_bank[pair] = project_pair(pair, ("g2", "neg_g1"))
             if n < PAIRS:
                 split_sides(n)
-            if phase == 1:
-                for group in round_groups:
-                    centre_weight(group)
+            if LNPOS == 1:
+                for group in at(n, 0):
+                    logarithm(group)
+            for group in at(n, QK):
+                centre_weight(group)
             if 1 <= n <= PAIRS:
                 pair = n - 1
-                group = pair // GROUP_PAIRS
-                if group >= VECTOR_GROUPS:
+                if pair // GROUP_PAIRS >= VECTOR_GROUPS:
                     gap_by_tensor(pair)
                 weigh_left(pair)
-                if n == 2:
-                    for side in SIDES:
-                        quantise_weight(side, "g2")
-                if phase == 1:
-                    if new_unit:
-                        quantise_unit(unit)
-                    if group > 0:
-                        subtract_mix(group - 1)
-                elif phase == 2:
-                    for old in round_groups:
-                        weigh_centre(old)
-                    add_right(group)
-                elif phase == 3:
-                    if new_unit:
-                        quantise_unit(unit)
-                    for old in round_groups:
-                        finish(old)
-                    subtract_mix(group - 1)
-                else:
-                    for old in round_pairs:
-                        subtract_e(old)
-                    add_right(group)
-                    for old in round_groups:
-                        subtract_log(old)
-        last = range(GROUPS - ROUND_GROUPS, GROUPS)
-        subtract_mix(GROUPS - 1)
-        for group in last:
-            weigh_centre(group)
-        for group in last:
-            finish(group)
+            if n == 1 and LATEC:
+                for side in SIDES:
+                    quantise_weight(side, "centre")
+            if n == G2N + 1:
+                for side in SIDES:
+                    quantise_weight(side, "g2")
+            if new_unit:
+                quantise_unit(unit)
+            for old in at(n, WK):
+                weigh_centre(old)
+            for old in es:
+                subtract_e(old)
+                if ADDR == 1 and old == es[min(2, len(es) - 1)] and n % 2 == 0 and 2 <= n <= PAIRS:
+                    add_right(n // 2 - 1)
+            if (not es or ADDR == 0) and n % 2 == 0 and 2 <= n <= PAIRS:
+                add_right(n // 2 - 1)
+            for old in es:
+                if old % GROUP_PAIRS == GROUP_PAIRS - 1:
+                    subtract_log(old // GROUP_PAIRS)
+            for old in at(n, FK):
+                finish(old)
+            if n % 2 == 1 and 3 <= n <= PAIRS + 1:
+                subtract_mix(n // 2 - 1)

@@ -23,30 +23,31 @@ GROUP_POSITIONS = 2 * GROUP_PAIRS
 GROUP_COLS = GROUP_PAIRS * PAIR_COLS
 GROUPS = PAIRS // GROUP_PAIRS
 ROUNDS = (2, 2, 2, 2)
-EP = 4
-EPL = 4
+EP = 8
+EPL = 8
 KEEP = 5
 WARM = 5
 LATEC = False
 GAPB = 3
-WB = 4
-SHB = 3
+ARG = ()
+WB = 3
+SHB = 4
 XB = 3
 FINE = {6: 2, 7: 2}
 GPC = 4
 DVG = 0
-SMG = ()
+SMG = range(2, 7)
 XV = [(2, u) for u in range(4, 10)]
 GV = (("c", 1),)
-LNPOS = 1
+LNPOS = 0
 CL = 2
 QK = 1
 WK = 2
 FK = 3
 G2N = 1
-EFIRST = 0
+EFIRST = 2
 ADDR = 1
-G0A = True
+G0A = False
 PIECE_BLOCKS = 2
 UNIT_BLOCKS = (1, 2, 2, 4, 4, 4, 4, 4, 4, 4)
 UNIT_FIRST = tuple(sum(UNIT_BLOCKS[:u]) for u in range(len(UNIT_BLOCKS)))
@@ -67,7 +68,7 @@ FLOPS = 2 * POSITIONS * P * (2 * K) * (4 * H)
 
 def tile_grconv_pa_t_kernel(tc, x, x_mix, WL, WR, GL, GR, out):
     nc = tc.nc
-    x_rows = x.rearrange("s a b k -> (a b) s k")
+    x_flat = x.rearrange("s a b k -> (s a b) k")
     mix_rows = x_mix.rearrange("s a b h -> (a b) s h")
     out_rows = out.rearrange("s a b h -> (a b) s h")
     centres = (WL, WR)
@@ -78,6 +79,7 @@ def tile_grconv_pa_t_kernel(tc, x, x_mix, WL, WR, GL, GR, out):
         const = ctx.enter_context(tc.tile_pool(name="const", bufs=1))
         resident = ctx.enter_context(tc.tile_pool(name="resident", bufs=1))
         stage = ctx.enter_context(tc.tile_pool(name="stage", bufs=2))
+        xp = ctx.enter_context(tc.tile_pool(name="xp", bufs=4))
         gapp = ctx.enter_context(tc.tile_pool(name="gapp", bufs=GAPB))
         wp = ctx.enter_context(tc.tile_pool(name="wp", bufs=4))
         weightp = ctx.enter_context(tc.tile_pool(name="weightp", bufs=WB))
@@ -99,13 +101,12 @@ def tile_grconv_pa_t_kernel(tc, x, x_mix, WL, WR, GL, GR, out):
         make_identity(nc, ident[:])
         neg_ident = const.tile([P, P], BF16)
 
-        x_nat = resident.tile([P, BLOCKS, K], BF16)
         mix_in = resident.tile([P, BLOCKS, H], BF16)
         x_codes = resident.tile([P, BLOCKS, P], U32, align_bytes=64)
         x_scales = resident.tile([P, BLOCKS, P], U8, align_bytes=64)
         w_codes = resident.tile([P, 2 * len(OPERANDS), H], U32, align_bytes=64)
         w_scales = resident.tile([P, 2 * len(OPERANDS), H], U8, align_bytes=64)
-        w_nat = {}
+        w_nat, x_nat = {}, {}
 
         def operand(side, name):
             return side * len(OPERANDS) + OPERANDS.index(name)
@@ -118,12 +119,14 @@ def tile_grconv_pa_t_kernel(tc, x, x_mix, WL, WR, GL, GR, out):
                 rows = centres[side]
             else:
                 rows = gates[side][GATE_CHUNK[chunk] * H : (GATE_CHUNK[chunk] + 1) * H, :]
-            w_nat[(side, chunk)] = resident.tile([P, H // P, K], BF16, name="w_nat_%d_%s" % (side, chunk))
-            nc.sync.dma_start(out=w_nat[(side, chunk)][:], in_=rows.rearrange("(t p) k -> p t k", p=P))
+            w_nat[(side, chunk)] = wp.tile([P, H // P, K], BF16, name="w_nat", tag="w_nat", bufs=6)
+            nc.sync.dma_start(out=w_nat[(side, chunk)][:], in_=rows.rearrange("(p t) k -> p t k", p=P))
 
         def load_x(unit):
             first, end = unit_span(unit)
-            nc.sync.dma_start(out=x_nat[:, first:end, :], in_=x_rows[:, first:end, :])
+            rows = x_flat[first * P : end * P, :]
+            x_nat[unit] = xp.tile([P, end - first, K], BF16, name="x_nat", tag="x_nat%d" % (end - first), bufs=min(end - first, 4))
+            nc.sync.dma_start(out=x_nat[unit][:], in_=rows.rearrange("(p t) k -> p t k", p=P))
 
         def load_mix(unit):
             first, end = unit_span(unit)
@@ -153,20 +156,21 @@ def tile_grconv_pa_t_kernel(tc, x, x_mix, WL, WR, GL, GR, out):
         def transpose_words(nat):
             tiles = nat.shape[1]
             nat_words = nat.bitcast(F32)
-            words = psum.tile([P, 2, tiles * P], F32, tag="bank")
+            words = psum.tile([P, 2, tiles, P], F32, tag="bank")
             for u in range(2):
                 for t in range(tiles):
                     nc.tensor.transpose(
-                        out=words[:, u, t * P : (t + 1) * P],
+                        out=words[:, u, t, :],
                         in_=nat_words[:, t, u : 2 * P : 2],
                         identity=ident_words[:],
                     )
             return words
 
-        def copy_words(copy, words, grouped):
+        def copy_words(copy, words, grouped, tiles, first):
+            end = first + words.shape[2]
             copy(
-                out=grouped.bitcast(F32).rearrange("p (r u) -> p r u", u=2),
-                in_=words[:].rearrange("p u r -> p r u"),
+                out=grouped.bitcast(F32).rearrange("p (r t u) -> p r t u", t=tiles, u=2)[:, :, first:end, :],
+                in_=words[:].rearrange("p u t r -> p r t u"),
             )
 
         def quantise(values, codes, scales):
@@ -179,7 +183,7 @@ def tile_grconv_pa_t_kernel(tc, x, x_mix, WL, WR, GL, GR, out):
 
         def copy_weight(copy, side, chunk):
             grouped = wp.tile([P, 4 * H], BF16, name="grouped", tag="w_grouped", align_bytes=64)
-            copy_words(copy, w_words[(side, chunk)], grouped[:])
+            copy_words(copy, w_words[(side, chunk)], grouped[:], H // P, 0)
             w_grouped[(side, chunk)] = grouped
 
         def turn_weight(side, chunk):
@@ -197,13 +201,14 @@ def tile_grconv_pa_t_kernel(tc, x, x_mix, WL, WR, GL, GR, out):
             return [(at, min(at + PIECE_BLOCKS, end)) for at in range(first, end, PIECE_BLOCKS)]
 
         def transpose_unit(unit):
-            x_words[unit] = [transpose_words(x_nat[:, at:to, :]) for at, to in unit_pieces(unit)]
+            first = UNIT_FIRST[unit]
+            x_words[unit] = [transpose_words(x_nat[unit][:, at - first : to - first, :]) for at, to in unit_pieces(unit)]
 
         def copy_unit(unit):
             first, end = unit_span(unit)
             x_grouped[unit] = stage.tile([P, 4 * P * (end - first)], BF16, name="x_grouped", tag="x_grouped", align_bytes=64, bufs=XB)
             for (at, to), words in zip(unit_pieces(unit), x_words[unit]):
-                copy_words(nc.vector.tensor_copy if unit in XV or (at - first, unit) in XV else nc.scalar.copy, words, x_grouped[unit][:, 4 * P * (at - first) : 4 * P * (to - first)])
+                copy_words(nc.vector.tensor_copy if unit in XV or (at - first, unit) in XV else nc.scalar.copy, words, x_grouped[unit][:], end - first, at - first)
 
         def quantise_unit(unit):
             first, end = unit_span(unit)
@@ -292,7 +297,7 @@ def tile_grconv_pa_t_kernel(tc, x, x_mix, WL, WR, GL, GR, out):
 
         def add_right(group):
             right = mixed(group * GROUP_POSITIONS + 1, GROUP_POSITIONS)
-            nc.vector.tensor_tensor(out=mix[group][:], in0=mix[group][:], in1=right, op=ALU.add)
+            (nc.gpsimd if group in ARG else nc.vector).tensor_tensor(out=mix[group][:], in0=mix[group][:], in1=right, op=ALU.add)
 
         def subtract_mix(group):
             if group in SMG:

@@ -29,7 +29,7 @@ KEEP = 5
 WARM = 5
 LATEC = False
 GAPB = 3
-ARG = ()
+ARG = (1, 3, 5, 7)
 WB = 3
 SHB = 4
 XB = 3
@@ -37,7 +37,7 @@ FINE = {6: 2, 7: 2}
 GPC = 4
 DVG = 0
 SMG = range(2, 7)
-XV = [(2, u) for u in range(4, 10)]
+XV = range(4, 10)
 GV = (("c", 1),)
 LNPOS = 0
 CL = 2

@@ -23,12 +23,21 @@ GROUP_POSITIONS = 2 * GROUP_PAIRS
 GROUP_COLS = GROUP_PAIRS * PAIR_COLS
 GROUPS = PAIRS // GROUP_PAIRS
 ROUNDS = (2, 2, 2, 2)
-EP = 8
-EPL = 8
+EP = 4
+EPL = 4
 KEEP = 5
 WARM = 5
 LATEC = False
 GAPB = 3
+CPOS = 1
+C3 = 0
+GH = 3
+CQ = 0
+SMH = 2
+ARH = 2
+UPAR = 1
+VORD = ("X", "W", "U", "WC", "SL", "AR", "Q", "F", "SM")
+RV = range(4, 12, 2)
 ARG = (1, 3, 5, 7)
 WB = 3
 SHB = 4
@@ -36,18 +45,18 @@ XB = 3
 FINE = {6: 2, 7: 2}
 GPC = 4
 DVG = 0
-SMG = range(2, 7)
-XV = range(4, 10)
-GV = (("c", 1),)
+SMG = range(0, 4)
+XV = range(4, 7)
+GV = ()
 LNPOS = 0
 CL = 2
 QK = 1
 WK = 2
 FK = 3
 G2N = 1
-EFIRST = 2
-ADDR = 1
-G0A = False
+EFIRST = 1
+ADDR = 0
+G0A = True
 PIECE_BLOCKS = 2
 UNIT_BLOCKS = (1, 2, 2, 4, 4, 4, 4, 4, 4, 4)
 UNIT_FIRST = tuple(sum(UNIT_BLOCKS[:u]) for u in range(len(UNIT_BLOCKS)))
@@ -284,7 +293,12 @@ def tile_grconv_pa_t_kernel(tc, x, x_mix, WL, WR, GL, GR, out):
             return [slice(i * GROUP_COLS // n, (i + 1) * GROUP_COLS // n) for i in range(n)]
 
         def hold_d(pair):
-            nc.scalar.activation(out=part(logit, pair), in_=d_bank[pair][:], func=AF.Relu, bias=plus_floor[:])
+            if pair in RV:
+                nc.vector.tensor_scalar(
+                    out=part(logit, pair), in0=d_bank[pair][:], scalar1=FLOOR, scalar2=0.0, op0=ALU.add, op1=ALU.max
+                )
+            else:
+                nc.scalar.activation(out=part(logit, pair), in_=d_bank[pair][:], func=AF.Relu, bias=plus_floor[:])
 
         def split_sides(pair):
             nc.scalar.activation(out=part(share, pair), in_=part(logit, pair), func=AF.Sigmoid, bias=minus_floor[:])
@@ -297,12 +311,18 @@ def tile_grconv_pa_t_kernel(tc, x, x_mix, WL, WR, GL, GR, out):
 
         def add_right(group):
             right = mixed(group * GROUP_POSITIONS + 1, GROUP_POSITIONS)
-            (nc.gpsimd if group in ARG else nc.vector).tensor_tensor(out=mix[group][:], in0=mix[group][:], in1=right, op=ALU.add)
+            if group in ARG:
+                for i in range(ARH):
+                    sl = slice(i * GROUP_COLS // ARH, (i + 1) * GROUP_COLS // ARH)
+                    nc.gpsimd.tensor_tensor(out=mix[group][:, sl], in0=mix[group][:, sl], in1=right[:, sl], op=ALU.add)
+            else:
+                nc.vector.tensor_tensor(out=mix[group][:], in0=mix[group][:], in1=right, op=ALU.add)
 
         def subtract_mix(group):
             if group in SMG:
-                for pair in range(group * GROUP_PAIRS, (group + 1) * GROUP_PAIRS):
-                    nc.gpsimd.tensor_tensor(out=part(centre, pair), in0=part(centre, pair), in1=part(mix, pair), op=ALU.subtract)
+                for i in range(SMH):
+                    sl = slice(i * GROUP_COLS // SMH, (i + 1) * GROUP_COLS // SMH)
+                    nc.gpsimd.tensor_tensor(out=centre[group][:, sl], in0=centre[group][:, sl], in1=mix[group][:, sl], op=ALU.subtract)
             else:
                 nc.vector.tensor_tensor(out=centre[group][:], in0=centre[group][:], in1=mix[group][:], op=ALU.subtract)
 
@@ -353,27 +373,35 @@ def tile_grconv_pa_t_kernel(tc, x, x_mix, WL, WR, GL, GR, out):
         quantise_unit(1)
         copy_weight(nc.vector.tensor_copy, RIGHT, "g1")
         for side in SIDES:
+            quantise_weight(side, "g1")
+        for side in SIDES:
             transpose_weight(side, "g0")
             copy_weight(nc.scalar.copy if side == LEFT or G0A else nc.vector.tensor_copy, side, "g0")
-        for side in SIDES:
-            quantise_weight(side, "g1")
         for side in SIDES:
             quantise_weight(side, "g0")
         transpose_unit(2)
         copy_unit(2)
         quantise_unit(2)
-        transpose_unit(3)
-        copy_unit(3)
-        if not LATEC:
+
+        def centre_operands():
             for side in SIDES:
                 transpose_weight(side, "centre")
                 copy_weight(nc.vector.tensor_copy if ("c", side) in GV else nc.scalar.copy, side, "centre")
-        for group in range(VECTOR_GROUPS):
-            gap_by_vector(group)
-        quantise_unit(3)
-        if not LATEC:
+
+        def centre_quantise():
             for side in SIDES:
                 quantise_weight(side, "centre")
+
+        transpose_unit(3)
+        if CPOS == 0:
+            centre_operands()
+        for group in range(min(GH, VECTOR_GROUPS)):
+            gap_by_vector(group)
+        if C3 == 0:
+            copy_unit(3)
+            quantise_unit(3)
+        if CPOS == 0:
+            centre_quantise()
 
         ends = {}
         first = 0
@@ -387,35 +415,37 @@ def tile_grconv_pa_t_kernel(tc, x, x_mix, WL, WR, GL, GR, out):
         def e_pairs(step):
             for end in ends:
                 k = step - end
-                per = EP if end < PAIRS else EPL
                 pairs = range(ends[end][0] * GROUP_PAIRS, end)
-                if 0 <= k and k * per < len(pairs):
-                    return list(pairs[k * per : (k + 1) * per])
+                if 0 <= k and k * EP < len(pairs):
+                    return list(pairs[k * EP : (k + 1) * EP])
             return []
 
+        nextu = HEAD_UNITS
         for n in range(PAIRS + 8):
-            unit = HEAD_UNITS + n // 2
-            new_unit = n % 2 == 1 and unit < UNITS
+            unit = nextu
+            new_unit = n >= 1 and n % 2 == UPAR and unit < UNITS
+            if new_unit:
+                nextu += 1
             es = e_pairs(n)
             if n < PAIRS:
                 if n % GROUP_PAIRS == 0:
                     open_group(n // GROUP_PAIRS)
                 if new_unit:
                     transpose_unit(unit)
-                    copy_unit(unit)
-                if n == 1 and LATEC:
-                    for side in SIDES:
-                        transpose_weight(side, "centre")
-                        copy_weight(nc.vector.tensor_copy if ("c", side) in GV else nc.scalar.copy, side, "centre")
+                    if unit not in XV:
+                        copy_unit(unit)
+                if n == 1 and CPOS == 2:
+                    centre_operands()
                 d_bank[n] = project_pair(n, ("g0", "neg_g1"))
                 hold_d(n)
-            if n == G2N:
+            if n == 0 and CPOS == 1:
+                centre_operands()
+            if n == 1:
                 for side in SIDES:
                     transpose_weight(side, "g2")
                     copy_weight(nc.vector.tensor_copy if ("g2", side) in GV else nc.scalar.copy, side, "g2")
-            if LNPOS == 0:
-                for group in at(n, 0):
-                    logarithm(group)
+            for group in at(n, 0):
+                logarithm(group)
             for pair in es[:EFIRST]:
                 e_bank[pair] = project_pair(pair, ("g2", "neg_g1"))
             if CL <= n < PAIRS + CL:
@@ -425,36 +455,47 @@ def tile_grconv_pa_t_kernel(tc, x, x_mix, WL, WR, GL, GR, out):
                 e_bank[pair] = project_pair(pair, ("g2", "neg_g1"))
             if n < PAIRS:
                 split_sides(n)
-            if LNPOS == 1:
-                for group in at(n, 0):
-                    logarithm(group)
+            if n == 0 and C3 == 1:
+                copy_unit(3)
+            if n == 0 and CPOS == 1 and CQ == 0:
+                centre_quantise()
+            if n == 0 and C3 == 1:
+                quantise_unit(3)
+            if n == 1 and (CPOS == 2 or CPOS == 1 and CQ == 1):
+                centre_quantise()
+            if n == 0:
+                for group in range(GH, VECTOR_GROUPS):
+                    gap_by_vector(group)
             for group in at(n, QK):
                 centre_weight(group)
-            if 1 <= n <= PAIRS:
-                pair = n - 1
-                if pair // GROUP_PAIRS >= VECTOR_GROUPS:
-                    gap_by_tensor(pair)
-                weigh_left(pair)
-            if n == 1 and LATEC:
-                for side in SIDES:
-                    quantise_weight(side, "centre")
-            if n == G2N + 1:
-                for side in SIDES:
-                    quantise_weight(side, "g2")
-            if new_unit:
-                quantise_unit(unit)
-            for old in at(n, WK):
-                weigh_centre(old)
-            for old in es:
-                subtract_e(old)
-                if ADDR == 1 and old == es[min(2, len(es) - 1)] and n % 2 == 0 and 2 <= n <= PAIRS:
+            for op in VORD:
+                if op == "X" and new_unit and unit in XV:
+                    copy_unit(unit)
+                elif op == "W":
+                    if 1 <= n <= PAIRS:
+                        pair = n - 1
+                        if pair // GROUP_PAIRS >= VECTOR_GROUPS:
+                            gap_by_tensor(pair)
+                        weigh_left(pair)
+                    if n == 2:
+                        for side in SIDES:
+                            quantise_weight(side, "g2")
+                elif op == "Q" and new_unit:
+                    quantise_unit(unit)
+                elif op == "WC":
+                    for old in at(n, WK):
+                        weigh_centre(old)
+                elif op == "U":
+                    for old in es:
+                        subtract_e(old)
+                elif op == "AR" and n % 2 == 0 and 2 <= n <= PAIRS:
                     add_right(n // 2 - 1)
-            if (not es or ADDR == 0) and n % 2 == 0 and 2 <= n <= PAIRS:
-                add_right(n // 2 - 1)
-            for old in es:
-                if old % GROUP_PAIRS == GROUP_PAIRS - 1:
-                    subtract_log(old // GROUP_PAIRS)
-            for old in at(n, FK):
-                finish(old)
-            if n % 2 == 1 and 3 <= n <= PAIRS + 1:
-                subtract_mix(n // 2 - 1)
+                elif op == "SL":
+                    for old in es:
+                        if old % GROUP_PAIRS == GROUP_PAIRS - 1:
+                            subtract_log(old // GROUP_PAIRS)
+                elif op == "F":
+                    for old in at(n, FK):
+                        finish(old)
+                elif op == "SM" and n % 2 == 1 and 3 <= n <= PAIRS + 1:
+                    subtract_mix(n // 2 - 1)

@@ -22,37 +22,41 @@ GROUP_PAIRS = 2
 GROUP_POSITIONS = 2 * GROUP_PAIRS
 GROUP_COLS = GROUP_PAIRS * PAIR_COLS
 GROUPS = PAIRS // GROUP_PAIRS
-ROUNDS = (2, 2, 2, 2)
+ROUNDS = (3, 3, 2)
 EP = 4
 EPL = 4
-KEEP = 5
+KEEP = 6
 WARM = 5
 LATEC = False
 GAPB = 3
-CPOS = 1
+CPOS = 0
+LORD = ("g10", "x0", "x1", "g11", "g00", "g01", "x2", "x3", "m0", "m1", "m2", "c0", "c1", "x4", "m3", "g20", "g21", "m4", "x5", "m5", "x6", "m6", "x7", "m7", "x8", "m8", "x9", "m9")
+PORD = ("T", "D", "E", "C", "G")
+AORD = ("X", "Q", "R", "LN", "SC", "SD")
+GLAG = 1
 C3 = 0
 GH = 3
 CQ = 0
 SMH = 2
 ARH = 2
-UPAR = 1
-VORD = ("X", "W", "U", "WC", "SL", "AR", "Q", "F", "SM")
-RV = range(4, 12, 2)
-ARG = (1, 3, 5, 7)
-WB = 3
+UPAR = 0
+VORD = ("X", "Q", "U", "W", "SL", "AR", "F", "WC", "SM")
+RV = (6, 7)
+ARG = (2, 4, 6)
+WB = 5
 SHB = 4
 XB = 3
 FINE = {6: 2, 7: 2}
 GPC = 4
 DVG = 0
-SMG = range(0, 4)
-XV = range(4, 7)
+SMG = (2, 4, 6)
+XV = (4,)
 GV = ()
 LNPOS = 0
 CL = 2
-QK = 1
+QK = 2
 WK = 2
-FK = 3
+FK = 5
 G2N = 1
 EFIRST = 1
 ADDR = 0
@@ -141,26 +145,13 @@ def tile_grconv_pa_t_kernel(tc, x, x_mix, WL, WR, GL, GR, out):
             first, end = unit_span(unit)
             nc.sync.dma_start(out=mix_in[:, first:end, :], in_=mix_rows[:, first:end, :])
 
-        load_weight(LEFT, "g1")
-        load_x(0)
-        load_x(1)
-        load_weight(RIGHT, "g1")
-        for side in SIDES:
-            load_weight(side, "g0")
-        load_x(2)
-        for unit in range(3):
-            load_mix(unit)
-        load_x(3)
-        for side in SIDES:
-            load_weight(side, "centre")
-        load_x(4)
-        load_mix(3)
-        for side in SIDES:
-            load_weight(side, "g2")
-        load_mix(4)
-        for unit in range(5, UNITS):
-            load_x(unit)
-            load_mix(unit)
+        for what in LORD:
+            if what[0] == "x":
+                load_x(int(what[1:]))
+            elif what[0] == "m":
+                load_mix(int(what[1:]))
+            else:
+                load_weight(int(what[-1]), {"c": "centre"}.get(what[:-1], what[:-1]))
 
         def transpose_words(nat):
             tiles = nat.shape[1]
@@ -427,56 +418,69 @@ def tile_grconv_pa_t_kernel(tc, x, x_mix, WL, WR, GL, GR, out):
             if new_unit:
                 nextu += 1
             es = e_pairs(n)
-            if n < PAIRS:
-                if n % GROUP_PAIRS == 0:
-                    open_group(n // GROUP_PAIRS)
-                if new_unit:
-                    transpose_unit(unit)
-                    if unit not in XV:
-                        copy_unit(unit)
-                if n == 1 and CPOS == 2:
-                    centre_operands()
-                d_bank[n] = project_pair(n, ("g0", "neg_g1"))
+            if n < PAIRS and n % GROUP_PAIRS == 0:
+                open_group(n // GROUP_PAIRS)
+            for op in PORD:
+                if op == "T":
+                    if new_unit:
+                        transpose_unit(unit)
+                    if n == 1 and CPOS == 2:
+                        centre_operands()
+                elif op == "D":
+                    if n < PAIRS:
+                        d_bank[n] = project_pair(n, ("g0", "neg_g1"))
+                    if n == 0 and CPOS == 1:
+                        for side in SIDES:
+                            transpose_weight(side, "centre")
+                    if n == 1:
+                        for side in SIDES:
+                            transpose_weight(side, "g2")
+                elif op == "E":
+                    for pair in es:
+                        e_bank[pair] = project_pair(pair, ("g2", "neg_g1"))
+                elif op == "C" and CL <= n < PAIRS + CL:
+                    c_bank[n - CL] = project_pair(n - CL, ("centre",))
+                elif op == "G" and 1 <= n - GLAG + 1 <= PAIRS:
+                    pair = n - GLAG
+                    if pair // GROUP_PAIRS >= VECTOR_GROUPS:
+                        gap_by_tensor(pair)
+            if n < PAIRS and n in RV:
                 hold_d(n)
-            if n == 0 and CPOS == 1:
-                centre_operands()
-            if n == 1:
-                for side in SIDES:
-                    transpose_weight(side, "g2")
-                    copy_weight(nc.vector.tensor_copy if ("g2", side) in GV else nc.scalar.copy, side, "g2")
-            for group in at(n, 0):
-                logarithm(group)
-            for pair in es[:EFIRST]:
-                e_bank[pair] = project_pair(pair, ("g2", "neg_g1"))
-            if CL <= n < PAIRS + CL:
-                c_bank[n - CL] = project_pair(n - CL, ("centre",))
-                squash_centre(n - CL)
-            for pair in es[EFIRST:]:
-                e_bank[pair] = project_pair(pair, ("g2", "neg_g1"))
-            if n < PAIRS:
-                split_sides(n)
-            if n == 0 and C3 == 1:
-                copy_unit(3)
+            for op in AORD:
+                if op == "X" and new_unit and unit not in XV:
+                    copy_unit(unit)
+                elif op == "R":
+                    if n < PAIRS and n not in RV:
+                        hold_d(n)
+                    if n == 0 and CPOS == 1:
+                        for side in SIDES:
+                            copy_weight(nc.vector.tensor_copy if ("c", side) in GV else nc.scalar.copy, side, "centre")
+                    if n == 1:
+                        for side in SIDES:
+                            copy_weight(nc.vector.tensor_copy if ("g2", side) in GV else nc.scalar.copy, side, "g2")
+                elif op == "LN":
+                    for group in at(n, 0):
+                        logarithm(group)
+                elif op == "SC" and CL <= n < PAIRS + CL:
+                    squash_centre(n - CL)
+                elif op == "SD" and n < PAIRS:
+                    split_sides(n)
+                elif op == "Q":
+                    for group in at(n, QK):
+                        centre_weight(group)
             if n == 0 and CPOS == 1 and CQ == 0:
                 centre_quantise()
-            if n == 0 and C3 == 1:
-                quantise_unit(3)
             if n == 1 and (CPOS == 2 or CPOS == 1 and CQ == 1):
                 centre_quantise()
             if n == 0:
                 for group in range(GH, VECTOR_GROUPS):
                     gap_by_vector(group)
-            for group in at(n, QK):
-                centre_weight(group)
             for op in VORD:
                 if op == "X" and new_unit and unit in XV:
                     copy_unit(unit)
                 elif op == "W":
                     if 1 <= n <= PAIRS:
-                        pair = n - 1
-                        if pair // GROUP_PAIRS >= VECTOR_GROUPS:
-                            gap_by_tensor(pair)
-                        weigh_left(pair)
+                        weigh_left(n - 1)
                     if n == 2:
                         for side in SIDES:
                             quantise_weight(side, "g2")

from contextlib import ExitStack

import concourse.mybir as mybir
from concourse.masks import make_identity

F32 = mybir.dt.float32
BF16 = mybir.dt.bfloat16
U32 = mybir.dt.uint32
U8 = mybir.dt.uint8
FP8X4 = mybir.dt.float8_e4m3fn_x4
AF = mybir.ActivationFunctionType
ALU = mybir.AluOpType

P = 128
K = 512
H = 256
POSITIONS = 32
BLOCKS = POSITIONS + 1
PAIR_COLS = 2 * H
PAIRS = POSITIONS // 2
GROUP_PAIRS = 2
GROUP_POSITIONS = 2 * GROUP_PAIRS
GROUP_COLS = GROUP_PAIRS * PAIR_COLS
GROUPS = PAIRS // GROUP_PAIRS
ROUNDS = (3, 3, 2)
EP = 4
EPL = 4
KEEP = 6
WARM = 5
LATEC = False
GAPB = 3
CPOS = 0
LORD = ("g10", "x0", "x1", "g11", "g00", "g01", "x2", "x3", "m0", "m1", "m2", "c0", "c1", "x4", "m3", "g20", "g21", "m4", "x5", "m5", "x6", "m6", "x7", "m7", "x8", "m8", "x9", "m9")
PORD = ("T", "D", "E", "C", "G")
AORD = ("X", "Q", "R", "LN", "SC", "SD")
GLAG = 1
C3 = 0
GH = 3
CQ = 0
SMH = 2
ARH = 2
UPAR = 0
VORD = ("X", "Q", "U", "W", "SL", "AR", "F", "WC", "SM")
RV = (6, 7)
ARG = (2, 4, 6)
WB = 5
SHB = 4
XB = 3
FINE = {6: 2, 7: 2}
GPC = 4
DVG = 0
SMG = (2, 4, 6)
XV = (4,)
GV = ()
LNPOS = 0
CL = 2
QK = 2
WK = 2
FK = 5
G2N = 1
EFIRST = 1
ADDR = 0
G0A = True
PIECE_BLOCKS = 2
UNIT_BLOCKS = (1, 2, 2, 4, 4, 4, 4, 4, 4, 4)
UNIT_FIRST = tuple(sum(UNIT_BLOCKS[:u]) for u in range(len(UNIT_BLOCKS)))
UNITS = len(UNIT_BLOCKS)
HEAD_UNITS = 4
VECTOR_GROUPS = 3
FLOOR = 40.0
PSUM_BANKS = 8

LEFT, RIGHT = 0, 1
SIDES = (LEFT, RIGHT)
OPERANDS = ("centre", "g0", "neg_g1", "g2")
CHUNKS = ("centre", "g0", "g1", "g2")
GATE_CHUNK = {"g0": 0, "g1": 1, "g2": 2}

FLOPS = 2 * POSITIONS * P * (2 * K) * (4 * H)


def tile_grconv_pa_t_kernel(tc, x, x_mix, WL, WR, GL, GR, out):
    nc = tc.nc
    x_flat = x.rearrange("s a b k -> (s a b) k")
    mix_rows = x_mix.rearrange("s a b h -> (a b) s h")
    out_rows = out.rearrange("s a b h -> (a b) s h")
    centres = (WL, WR)
    gates = (GL, GR)

    with ExitStack() as ctx:
        ctx.enter_context(tc.manual_schedule())
        const = ctx.enter_context(tc.tile_pool(name="const", bufs=1))
        resident = ctx.enter_context(tc.tile_pool(name="resident", bufs=1))
        stage = ctx.enter_context(tc.tile_pool(name="stage", bufs=2))
        xp = ctx.enter_context(tc.tile_pool(name="xp", bufs=4))
        gapp = ctx.enter_context(tc.tile_pool(name="gapp", bufs=GAPB))
        wp = ctx.enter_context(tc.tile_pool(name="wp", bufs=4))
        weightp = ctx.enter_context(tc.tile_pool(name="weightp", bufs=WB))
        sharep = ctx.enter_context(tc.tile_pool(name="sharep", bufs=SHB))
        keep = ctx.enter_context(tc.tile_pool(name="keep", bufs=KEEP))
        psum = ctx.enter_context(tc.psum_pool(name="psum", bufs=PSUM_BANKS))

        zeros = const.tile([P, PAIR_COLS], BF16)
        nc.vector.memset(zeros[:], 0.0)
        plus_floor = const.tile([P, 1], F32)
        nc.vector.memset(plus_floor[:], FLOOR)
        minus_floor = const.tile([P, 1], F32)
        nc.vector.memset(minus_floor[:], -FLOOR)
        warm = const.tile([P, 1], F32)
        nc.scalar.activation(out=warm[:], in_=plus_floor[:], func=AF.Sigmoid)
        ident_words = const.tile([P, P], F32)
        make_identity(nc, ident_words[:])
        ident = const.tile([P, P], BF16)
        make_identity(nc, ident[:])
        neg_ident = const.tile([P, P], BF16)

        mix_in = resident.tile([P, BLOCKS, H], BF16)
        x_codes = resident.tile([P, BLOCKS, P], U32, align_bytes=64)
        x_scales = resident.tile([P, BLOCKS, P], U8, align_bytes=64)
        w_codes = resident.tile([P, 2 * len(OPERANDS), H], U32, align_bytes=64)
        w_scales = resident.tile([P, 2 * len(OPERANDS), H], U8, align_bytes=64)
        w_nat, x_nat = {}, {}

        def operand(side, name):
            return side * len(OPERANDS) + OPERANDS.index(name)

        def unit_span(unit):
            return UNIT_FIRST[unit], UNIT_FIRST[unit] + UNIT_BLOCKS[unit]

        def load_weight(side, chunk):
            if chunk == "centre":
                rows = centres[side]
            else:
                rows = gates[side][GATE_CHUNK[chunk] * H : (GATE_CHUNK[chunk] + 1) * H, :]
            w_nat[(side, chunk)] = wp.tile([P, H // P, K], BF16, name="w_nat", tag="w_nat", bufs=6)
            nc.sync.dma_start(out=w_nat[(side, chunk)][:], in_=rows.rearrange("(p t) k -> p t k", p=P))

        def load_x(unit):
            first, end = unit_span(unit)
            rows = x_flat[first * P : end * P, :]
            x_nat[unit] = xp.tile([P, end - first, K], BF16, name="x_nat", tag="x_nat%d" % (end - first), bufs=min(end - first, 4))
            nc.sync.dma_start(out=x_nat[unit][:], in_=rows.rearrange("(p t) k -> p t k", p=P))

        def load_mix(unit):
            first, end = unit_span(unit)
            nc.sync.dma_start(out=mix_in[:, first:end, :], in_=mix_rows[:, first:end, :])

        for what in LORD:
            if what[0] == "x":
                load_x(int(what[1:]))
            elif what[0] == "m":
                load_mix(int(what[1:]))
            else:
                load_weight(int(what[-1]), {"c": "centre"}.get(what[:-1], what[:-1]))

        def transpose_words(nat):
            tiles = nat.shape[1]
            nat_words = nat.bitcast(F32)
            words = psum.tile([P, 2, tiles, P], F32, tag="bank")
            for u in range(2):
                for t in range(tiles):
                    nc.tensor.transpose(
                        out=words[:, u, t, :],
                        in_=nat_words[:, t, u : 2 * P : 2],
                        identity=ident_words[:],
                    )
            return words

        def copy_words(copy, words, grouped, tiles, first):
            end = first + words.shape[2]
            copy(
                out=grouped.bitcast(F32).rearrange("p (r t u) -> p r t u", t=tiles, u=2)[:, :, first:end, :],
                in_=words[:].rearrange("p u t r -> p r t u"),
            )

        def quantise(values, codes, scales):
            nc.vector.quantize_mx(out=codes.bitcast(FP8X4), scales=scales, in_=values)

        w_words, w_grouped = {}, {}

        def transpose_weight(side, chunk):
            w_words[(side, chunk)] = transpose_words(w_nat[(side, chunk)][:])

        def copy_weight(copy, side, chunk):
            grouped = wp.tile([P, 4 * H], BF16, name="grouped", tag="w_grouped", align_bytes=64)
            copy_words(copy, w_words[(side, chunk)], grouped[:], H // P, 0)
            w_grouped[(side, chunk)] = grouped

        def turn_weight(side, chunk):
            nat = w_nat[(side, chunk)][:].rearrange("p t k -> p (t k)")
            nc.vector.tensor_scalar_mul(out=nat, in0=nat, scalar1=-1.0)

        def quantise_weight(side, chunk):
            w = operand(side, OPERANDS[CHUNKS.index(chunk)])
            quantise(w_grouped[(side, chunk)][:], w_codes[:, w, :], w_scales[:, w, :])

        x_words, x_grouped = {}, {}

        def unit_pieces(unit):
            first, end = unit_span(unit)
            return [(at, min(at + PIECE_BLOCKS, end)) for at in range(first, end, PIECE_BLOCKS)]

        def transpose_unit(unit):
            first = UNIT_FIRST[unit]
            x_words[unit] = [transpose_words(x_nat[unit][:, at - first : to - first, :]) for at, to in unit_pieces(unit)]

        def copy_unit(unit):
            first, end = unit_span(unit)
            x_grouped[unit] = stage.tile([P, 4 * P * (end - first)], BF16, name="x_grouped", tag="x_grouped", align_bytes=64, bufs=XB)
            for (at, to), words in zip(unit_pieces(unit), x_words[unit]):
                copy_words(nc.vector.tensor_copy if unit in XV or (at - first, unit) in XV else nc.scalar.copy, words, x_grouped[unit][:], end - first, at - first)

        def quantise_unit(unit):
            first, end = unit_span(unit)
            quantise(
                x_grouped[unit][:],
                x_codes[:, first:end, :].rearrange("p s r -> p (s r)"),
                x_scales[:, first:end, :].rearrange("p s r -> p (s r)"),
            )

        def project(acc, block, names):
            passes = [(block + side, operand(side, name)) for side in SIDES for name in names]
            for n, (x_block, w) in enumerate(passes):
                nc.tensor.matmul_mx(
                    out=acc,
                    lhsT=x_codes[:, x_block, :].bitcast(FP8X4),
                    lhsT_scale=x_scales[:, x_block, :],
                    rhs=w_codes[:, w, :].bitcast(FP8X4),
                    rhs_scale=w_scales[:, w, :],
                    start=(n == 0),
                    stop=(n == len(passes) - 1),
                )

        def new_bank():
            return psum.tile([P, PAIR_COLS], F32, name="bank", tag="bank")

        def project_pair(pair, names):
            bank = new_bank()
            for half in range(2):
                project(bank[:, half * H : (half + 1) * H], 2 * pair + half, names)
            return bank

        def mixed(first, count):
            return mix_in[:, first : first + count, :].rearrange("p s h -> p (s h)")

        def part(tiles, pair):
            at = (pair % GROUP_PAIRS) * PAIR_COLS
            return tiles[pair // GROUP_PAIRS][:, at : at + PAIR_COLS]

        d_bank, c_bank, e_bank, gap = {}, {}, {}, {}
        gap_tile = {}
        centre, share, logit, mix, weight = {}, {}, {}, {}, {}

        def open_group(group):
            for tiles, pool, name in (
                (share, sharep, "share"),
                (centre, keep, "centre"),
                (logit, keep, "logit"),
                (mix, keep, "mix"),
            ):
                tiles[group] = pool.tile([P, GROUP_COLS], F32, name=name, tag=name)

        def gap_by_vector(group):
            first = group * GROUP_POSITIONS
            gap_tile[group] = gapp.tile([P, GROUP_COLS], F32, name="gap", tag="gap")
            for s in range(0, GROUP_POSITIONS, GPC):
                (nc.gpsimd if DVG else nc.vector).tensor_tensor(
                    out=gap_tile[group][:, s * H : (s + GPC) * H],
                    in0=mixed(first + s, GPC),
                    in1=mixed(first + s + 1, GPC),
                    op=ALU.subtract,
                )
            for pair in range(group * GROUP_PAIRS, (group + 1) * GROUP_PAIRS):
                gap[pair] = part(gap_tile, pair)

        def gap_by_tensor(pair):
            bank = new_bank()
            nc.tensor.matmul(out=bank[:], lhsT=ident[:], rhs=mixed(2 * pair, 2), start=True, stop=False)
            nc.tensor.matmul(out=bank[:], lhsT=neg_ident[:], rhs=mixed(2 * pair + 1, 2), start=False, stop=True)
            gap[pair] = bank[:]

        def cuts(group):
            n = FINE.get(group, 1)
            return [slice(i * GROUP_COLS // n, (i + 1) * GROUP_COLS // n) for i in range(n)]

        def hold_d(pair):
            if pair in RV:
                nc.vector.tensor_scalar(
                    out=part(logit, pair), in0=d_bank[pair][:], scalar1=FLOOR, scalar2=0.0, op0=ALU.add, op1=ALU.max
                )
            else:
                nc.scalar.activation(out=part(logit, pair), in_=d_bank[pair][:], func=AF.Relu, bias=plus_floor[:])

        def split_sides(pair):
            nc.scalar.activation(out=part(share, pair), in_=part(logit, pair), func=AF.Sigmoid, bias=minus_floor[:])

        def squash_centre(pair):
            nc.scalar.activation(out=part(centre, pair), in_=c_bank[pair][:], func=AF.Sigmoid)

        def weigh_left(pair):
            nc.vector.tensor_tensor(out=part(mix, pair), in0=part(share, pair), in1=gap[pair], op=ALU.mult)

        def add_right(group):
            right = mixed(group * GROUP_POSITIONS + 1, GROUP_POSITIONS)
            if group in ARG:
                for i in range(ARH):
                    sl = slice(i * GROUP_COLS // ARH, (i + 1) * GROUP_COLS // ARH)
                    nc.gpsimd.tensor_tensor(out=mix[group][:, sl], in0=mix[group][:, sl], in1=right[:, sl], op=ALU.add)
            else:
                nc.vector.tensor_tensor(out=mix[group][:], in0=mix[group][:], in1=right, op=ALU.add)

        def subtract_mix(group):
            if group in SMG:
                for i in range(SMH):
                    sl = slice(i * GROUP_COLS // SMH, (i + 1) * GROUP_COLS // SMH)
                    nc.gpsimd.tensor_tensor(out=centre[group][:, sl], in0=centre[group][:, sl], in1=mix[group][:, sl], op=ALU.subtract)
            else:
                nc.vector.tensor_tensor(out=centre[group][:], in0=centre[group][:], in1=mix[group][:], op=ALU.subtract)

        def logarithm(group):
            weight[group] = weightp.tile([P, GROUP_COLS], F32, name="weight", tag="weight")
            for sl in cuts(group):
                nc.scalar.activation(out=weight[group][:, sl], in_=share[group][:, sl], func=AF.Ln)

        def subtract_e(pair):
            nc.vector.tensor_tensor(out=part(logit, pair), in0=part(logit, pair), in1=e_bank[pair][:], op=ALU.subtract)

        def subtract_log(group):
            for sl in cuts(group):
                nc.vector.tensor_tensor(out=logit[group][:, sl], in0=logit[group][:, sl], in1=weight[group][:, sl], op=ALU.subtract)

        def centre_weight(group):
            for sl in cuts(group):
                nc.scalar.activation(out=weight[group][:, sl], in_=logit[group][:, sl], func=AF.Sigmoid, scale=-1.0, bias=plus_floor[:])

        def weigh_centre(group):
            for sl in cuts(group):
                nc.vector.tensor_tensor(out=centre[group][:, sl], in0=centre[group][:, sl], in1=weight[group][:, sl], op=ALU.mult)

        def finish(group):
            first = group * GROUP_POSITIONS
            for i, sl in enumerate(cuts(group)):
                nc.vector.tensor_tensor(out=centre[group][:, sl], in0=centre[group][:, sl], in1=mix[group][:, sl], op=ALU.add)
                w = GROUP_POSITIONS // len(cuts(group))
                nc.sync.dma_start(
                    out=out_rows[:, first + i * w : first + (i + 1) * w, :],
                    in_=centre[group][:, sl].rearrange("p (s h) -> p s h", s=w),
                )

        if WARM:
            bank = new_bank()
            for n in range(WARM):
                nc.tensor.matmul(out=bank[:], lhsT=zeros[:, :P], rhs=zeros[:], start=True, stop=True)
        for unit in range(2):
            transpose_unit(unit)
            copy_unit(unit)
        turn_weight(LEFT, "g1")
        turn_weight(RIGHT, "g1")
        nc.vector.tensor_scalar_mul(out=neg_ident[:], in0=ident[:], scalar1=-1.0)
        for side in SIDES:
            transpose_weight(side, "g1")
        copy_weight(nc.scalar.copy, LEFT, "g1")
        quantise_unit(0)
        quantise_unit(1)
        copy_weight(nc.vector.tensor_copy, RIGHT, "g1")
        for side in SIDES:
            quantise_weight(side, "g1")
        for side in SIDES:
            transpose_weight(side, "g0")
            copy_weight(nc.scalar.copy if side == LEFT or G0A else nc.vector.tensor_copy, side, "g0")
        for side in SIDES:
            quantise_weight(side, "g0")
        transpose_unit(2)
        copy_unit(2)
        quantise_unit(2)

        def centre_operands():
            for side in SIDES:
                transpose_weight(side, "centre")
                copy_weight(nc.vector.tensor_copy if ("c", side) in GV else nc.scalar.copy, side, "centre")

        def centre_quantise():
            for side in SIDES:
                quantise_weight(side, "centre")

        transpose_unit(3)
        if CPOS == 0:
            centre_operands()
        for group in range(min(GH, VECTOR_GROUPS)):
            gap_by_vector(group)
        if C3 == 0:
            copy_unit(3)
            quantise_unit(3)
        if CPOS == 0:
            centre_quantise()

        ends = {}
        first = 0
        for size in ROUNDS:
            ends[(first + size) * GROUP_PAIRS] = list(range(first, first + size))
            first += size

        def at(step, lag):
            return ends.get(step - lag, [])

        def e_pairs(step):
            for end in ends:
                k = step - end
                pairs = range(ends[end][0] * GROUP_PAIRS, end)
                if 0 <= k and k * EP < len(pairs):
                    return list(pairs[k * EP : (k + 1) * EP])
            return []

        nextu = HEAD_UNITS
        for n in range(PAIRS + 8):
            unit = nextu
            new_unit = n >= 1 and n % 2 == UPAR and unit < UNITS
            if new_unit:
                nextu += 1
            es = e_pairs(n)
            if n < PAIRS and n % GROUP_PAIRS == 0:
                open_group(n // GROUP_PAIRS)
            for op in PORD:
                if op == "T":
                    if new_unit:
                        transpose_unit(unit)
                    if n == 1 and CPOS == 2:
                        centre_operands()
                elif op == "D":
                    if n < PAIRS:
                        d_bank[n] = project_pair(n, ("g0", "neg_g1"))
                    if n == 0 and CPOS == 1:
                        for side in SIDES:
                            transpose_weight(side, "centre")
                    if n == 1:
                        for side in SIDES:
                            transpose_weight(side, "g2")
                elif op == "E":
                    for pair in es:
                        e_bank[pair] = project_pair(pair, ("g2", "neg_g1"))
                elif op == "C" and CL <= n < PAIRS + CL:
                    c_bank[n - CL] = project_pair(n - CL, ("centre",))
                elif op == "G" and 1 <= n - GLAG + 1 <= PAIRS:
                    pair = n - GLAG
                    if pair // GROUP_PAIRS >= VECTOR_GROUPS:
                        gap_by_tensor(pair)
            if n < PAIRS and n in RV:
                hold_d(n)
            for op in AORD:
                if op == "X" and new_unit and unit not in XV:
                    copy_unit(unit)
                elif op == "R":
                    if n < PAIRS and n not in RV:
                        hold_d(n)
                    if n == 0 and CPOS == 1:
                        for side in SIDES:
                            copy_weight(nc.vector.tensor_copy if ("c", side) in GV else nc.scalar.copy, side, "centre")
                    if n == 1:
                        for side in SIDES:
                            copy_weight(nc.vector.tensor_copy if ("g2", side) in GV else nc.scalar.copy, side, "g2")
                elif op == "LN":
                    for group in at(n, 0):
                        logarithm(group)
                elif op == "SC" and CL <= n < PAIRS + CL:
                    squash_centre(n - CL)
                elif op == "SD" and n < PAIRS:
                    split_sides(n)
                elif op == "Q":
                    for group in at(n, QK):
                        centre_weight(group)
            if n == 0 and CPOS == 1 and CQ == 0:
                centre_quantise()
            if n == 1 and (CPOS == 2 or CPOS == 1 and CQ == 1):
                centre_quantise()
            if n == 0:
                for group in range(GH, VECTOR_GROUPS):
                    gap_by_vector(group)
            for op in VORD:
                if op == "X" and new_unit and unit in XV:
                    copy_unit(unit)
                elif op == "W":
                    if 1 <= n <= PAIRS:
                        weigh_left(n - 1)
                    if n == 2:
                        for side in SIDES:
                            quantise_weight(side, "g2")
                elif op == "Q" and new_unit:
                    quantise_unit(unit)
                elif op == "WC":
                    for old in at(n, WK):
                        weigh_centre(old)
                elif op == "U":
                    for old in es:
                        subtract_e(old)
                elif op == "AR" and n % 2 == 0 and 2 <= n <= PAIRS:
                    add_right(n // 2 - 1)
                elif op == "SL":
                    for old in es:
                        if old % GROUP_PAIRS == GROUP_PAIRS - 1:
                            subtract_log(old // GROUP_PAIRS)
                elif op == "F":
                    for old in at(n, FK):
                        finish(old)
                elif op == "SM" and n % 2 == 1 and 3 <= n <= PAIRS + 1:
                    subtract_mix(n // 2 - 1)
